import numpy as np
import ml_dtypes


def mxq(x, axis, fmt="e4m3"):
    dtype, down = {"e4m3": (ml_dtypes.float8_e4m3fn, 7), "e5m2": (ml_dtypes.float8_e5m2, 14)}[fmt]
    v = np.moveaxis(np.asarray(x, np.float32).astype(ml_dtypes.bfloat16).astype(np.float64), axis, -1)
    blocks = v.reshape(v.shape[:-1] + (-1, 32))
    amax = np.abs(blocks).max(-1, keepdims=True)
    byte = np.maximum(np.where(amax > 0, np.frexp(amax)[1] - 1 + 127, 0) - down, 1)
    scale = np.exp2(byte - 127.0)
    codes = (blocks / scale).astype(np.float32).astype(dtype).astype(np.float64)
    return np.moveaxis((codes * scale).reshape(v.shape), -1, axis)


WIDE = False


def mx_kscale(k):
    if not WIDE:
        return np.ones(k)
    levels = np.array([10, -10, 5, -5, 0])
    if k % 512:
        return np.exp2(np.random.permutation(np.resize(levels, k // 32))).repeat(32)
    a = np.empty((k // 512, 16))
    for p in range(k // 512):
        a[p, :8] = np.random.permutation(np.resize(levels, 8))
        for g in range(8):
            far = levels[np.abs(levels - a[p, g]) >= 10]
            a[p, g + 8] = far[np.random.randint(len(far))]
    return np.exp2(a.ravel()).repeat(32)


BF16 = ml_dtypes.bfloat16


def bf(x):
    return np.asarray(x, np.float32).astype(BF16)


def f64(x):
    return np.asarray(x).astype(np.float64)


B, S, HID, H, KV, D, T = 4, 2048, 1024, 2, 1, 64, 2048
DQ = H * D
DKV = KV * D
OUT = DQ + 2 * DKV
THETA = 1e4


def make_pos_emb():
    i = np.repeat(np.arange(D // 2), 2)
    freq = np.power(THETA, -i * 2.0 / D)
    t = freq[:, None] * f64(np.arange(T))[None, :]
    cos = np.cos(t)
    sin = np.sin(t)
    sin[0::2] *= -1.0
    return np.concatenate([cos, sin], axis=0).T


def flip_pairs(x):
    return x.reshape(x.shape[:-1] + (D // 2, 2))[..., ::-1].reshape(x.shape)


def apply_rope(x, pe):
    return x * pe[:, :D] + flip_pairs(x) * pe[:, D:]


def setup_inputs():
    s = mx_kscale(HID)
    return {"tensor": bf(np.random.standard_normal((B, S, HID)) * s),
            "w_qkv": bf(np.random.standard_normal((OUT, HID)) * 1.5 / np.sqrt(HID) / s[None, :]),
            "b_qkv": bf(np.random.standard_normal(OUT) * 0.3),
            "pos_emb": bf(make_pos_emb())}


def reference(tensor, w_qkv, b_qkv, pos_emb):
    qkv = (mxq(f64(tensor), 2, "e4m3") @ mxq(f64(w_qkv), 1, "e4m3").T) + f64(b_qkv)
    q = qkv[..., :DQ].reshape(B, S, H, D).transpose(0, 2, 1, 3)
    k = qkv[..., DQ:DQ + DKV].reshape(B, S, KV, D).transpose(0, 2, 1, 3)
    v = qkv[..., DQ + DKV:].reshape(B, S, KV, D).transpose(0, 2, 1, 3)
    pe = f64(pos_emb)[:S]
    return apply_rope(q, pe), apply_rope(k, pe), v

@@ -1,0 +1,235 @@
+from contextlib import ExitStack
+
+import concourse.mybir as mybir
+from concourse.masks import make_identity
+
+FLOPS = 2 * 8192 * 1024 * 256
+
+F32 = mybir.dt.float32
+BF16 = mybir.dt.bfloat16
+U32 = mybir.dt.uint32
+U8 = mybir.dt.uint8
+FP8X4 = mybir.dt.float8_e4m3fn_x4
+ADD = mybir.AluOpType.add
+MULT = mybir.AluOpType.mult
+IDENT = mybir.ActivationFunctionType.Identity
+
+P = 128
+NB = 4
+TPP = 16
+HID = 1024
+UPB = TPP // 2
+NU = NB * UPB
+
+MANUAL = True
+V_COPY_ON_VECTOR = True
+TAIL_ON_VECTOR = True
+
+
+def tile_multiqueryattention_pa_t_kernel(tc, tensor, w_qkv, b_qkv, pos_emb, out_0, out_1, out_2):
+    nc = tc.nc
+    with ExitStack() as ctx:
+        const = ctx.enter_context(tc.tile_pool(name="const", bufs=1))
+        xpool = ctx.enter_context(tc.tile_pool(name="xpool", bufs=1))
+        gpool = ctx.enter_context(tc.tile_pool(name="gpool", bufs=2))
+        cpool = ctx.enter_context(tc.tile_pool(name="cpool", bufs=2))
+        epool = ctx.enter_context(tc.tile_pool(name="epool", bufs=2))
+        mpool = ctx.enter_context(tc.tile_pool(name="mpool", bufs=4))
+        ypool = ctx.enter_context(tc.tile_pool(name="ypool", bufs=3))
+        psum = ctx.enter_context(tc.psum_pool(name="psum", bufs=1))
+        if MANUAL:
+            ctx.enter_context(tc.manual_schedule())
+
+        groups = [[0], [1]] + [[n, n + 1] for n in range(2, NU, 2)]
+        NG = len(groups)
+        group_index = {}
+        for k in range(NG):
+            for n in groups[k]:
+                group_index[n] = k
+
+        bb = const.tile([P, 256], BF16, name="bb")
+        nc.scalar.dma_start(out=bb[:], in_=b_qkv.partition_broadcast(P))
+        w_sb = const.tile([P, 2, HID], BF16, name="w_sb")
+        nc.sync.dma_start(out=w_sb[:], in_=w_qkv.rearrange("(a p) k -> p a k", p=P))
+        xsrc = {}
+
+        def load_x(n0, units):
+            b = n0 // UPB
+            t0 = 2 * (n0 % UPB)
+            view = tensor[b].rearrange("(p t) k -> p t k", t=TPP)
+            xt = xpool.tile([P, 2 * units, HID], BF16, name="x%d" % n0)
+            nc.sync.dma_start(out=xt[:], in_=view[:, t0:t0 + 2 * units, :])
+            for j in range(2 * units):
+                xsrc[(n0 + j // 2, j % 2)] = xt[:, j, :]
+
+        load_x(0, 1)
+        load_x(1, 1)
+        pe_sb = const.tile([P, TPP, 128], BF16, name="pe_sb")
+        nc.sync.dma_start(out=pe_sb[:], in_=pos_emb.rearrange("(p t) c -> p t c", t=TPP))
+        for n0 in range(2, NU, 2):
+            load_x(n0, 2)
+
+        ident_f = const.tile([P, P], F32, name="ident_f")
+        make_identity(nc, ident_f[:])
+
+        bsel = const.tile([P, 2, P], F32, name="bsel")
+        nc.vector.tensor_tensor(
+            out=bsel[:], in0=bb[:].rearrange("p (f j) -> p f j", f=2),
+            in1=ident_f[:].unsqueeze(1).to_broadcast([P, 2, P]), op=MULT)
+        bcol = const.tile([P, 2], F32, name="bcol")
+        nc.vector.tensor_reduce(out=bcol[:], in_=bsel[:], axis=mybir.AxisListType.X, op=ADD)
+
+        tab = const.tile([P, TPP, 2, 64], BF16, name="tab")
+
+        def build_tab(ta0, ta1):
+            cos_src = pe_sb[:, ta0:ta1, 0:64]
+            sin_src = pe_sb[:, ta0:ta1, 64:128].rearrange("p t (i e) -> p t i e", e=2)[:, :, :, ::-1]
+            sin_dst = tab[:, ta0:ta1, 1, :].rearrange("p t (i e) -> p t i e", e=2)
+            nc.gpsimd.tensor_scalar(out=tab[:, ta0:ta1, 0, :], in0=cos_src, scalar1=1.0, scalar2=0.0,
+                                    op0=MULT, op1=ADD)
+            nc.gpsimd.tensor_scalar(out=sin_dst, in0=sin_src, scalar1=1.0, scalar2=0.0, op0=MULT, op1=ADD)
+
+        build_tab(0, 4)
+        build_tab(4, TPP)
+
+        wg = const.tile([P, 2048], BF16, name="wg", align_bytes=64)
+        wg_f = wg[:].bitcast(F32).rearrange("p (g n u) -> p g n u", g=2, u=2)
+        for a in range(2):
+            tw = psum.tile([P, 512], F32, tag="T%d" % (2 + a), name="tw%d" % a)
+            wa = w_sb[:, a, :].bitcast(F32)
+            for q in range(4):
+                nc.tensor.transpose(tw[:, 128 * q:128 * (q + 1)], wa[:, 256 * (q // 2) + q % 2:256 * (q // 2 + 1):2], ident_f[:])
+            src = tw[:].rearrange("p (g u n) -> p g n u", g=2, u=2)
+            if a == 0:
+                nc.scalar.copy(out=wg_f[:, :, 0:128, :], in_=src)
+            else:
+                nc.vector.tensor_copy(out=wg_f[:, :, 128:256, :], in_=src)
+        wc = const.tile([P, 512], U32, name="wc", align_bytes=64)
+        ws = const.tile([P, 512], U8, name="ws", align_bytes=64)
+        nc.vector.quantize_mx(out=wc[:].bitcast(FP8X4), scales=ws[:], in_=wg[:])
+
+        tbank = {}
+        grp = {}
+        codes = {}
+        fbank = {}
+        xtb = {}
+        ybank = {}
+        work = {}
+        ystage = {}
+
+        def transposes(k):
+            for n in groups[k]:
+                for tt in range(2):
+                    tp = psum.tile([P, 512], F32, tag="T%d" % ((2 * n + tt) % 4), name="T%d_%d" % (tt, n))
+                    xa = xsrc[(n, tt)].bitcast(F32)
+                    for q in range(4):
+                        nc.tensor.transpose(tp[:, 128 * q:128 * (q + 1)], xa[:, 256 * (q // 2) + q % 2:256 * (q // 2 + 1):2], ident_f[:])
+                    tbank[(n, tt)] = tp
+
+        def copies(k):
+            tiles = 2 * len(groups[k])
+            g = gpool.tile([P, tiles * HID], BF16, tag="grp", name="grp%d" % k, align_bytes=64)
+            gf = g[:].bitcast(F32).rearrange("p (g i r u) -> p g i r u", g=2, i=tiles, u=2)
+            for n in groups[k]:
+                for tt in range(2):
+                    nc.scalar.copy(out=gf[:, :, 2 * (n - groups[k][0]) + tt],
+                                   in_=tbank[(n, tt)][:].rearrange("p (g u r) -> p g r u", g=2, u=2))
+            grp[k] = g
+
+        def quant(k):
+            tiles = 2 * len(groups[k])
+            c = cpool.tile([P, tiles * 256], U32, tag="codes", name="codes%d" % k, align_bytes=64)
+            s = cpool.tile([P, tiles * 256], U8, tag="scl", name="scl%d" % k, align_bytes=64)
+            nc.vector.quantize_mx(out=c[:].bitcast(FP8X4), scales=s[:], in_=grp[k][:])
+            codes[k] = (c, s)
+
+        def mx(k):
+            c, s = codes[k]
+            ntok = 256 * len(groups[k])
+            for f in range(2):
+                fb = psum.tile([P, ntok], F32, tag="F%d" % f, name="F%d_%d" % (f, k))
+                for g in range(2):
+                    lo = 256 * g + 128 * f
+                    nc.tensor.matmul_mx(
+                        out=fb[:],
+                        lhsT=wc[:, lo:lo + 128].bitcast(FP8X4), lhsT_scale=ws[:, lo:lo + 128],
+                        rhs=c[:, ntok * g:ntok * (g + 1)].bitcast(FP8X4), rhs_scale=s[:, ntok * g:ntok * (g + 1)],
+                        start=(g == 0), stop=(g == 1))
+                fbank[(k, f)] = fb
+
+        def evac(k):
+            ntok = 256 * len(groups[k])
+            for f in range(2):
+                xt = epool.tile([P, ntok], F32, tag="xtb%d" % f, name="xtb%d_%d" % (f, k))
+                nc.scalar.activation(out=xt[:], in_=fbank[(k, f)][:], func=IDENT, bias=bcol[:, f:f + 1], scale=1.0)
+                xtb[(k, f)] = xt
+
+        def back(n):
+            k = group_index[n]
+            yb = psum.tile([P, 2, 256], F32, tag="Y%d" % (n % 2), name="Y_%d" % n)
+            for tt in range(2):
+                lo = 128 * (2 * (n - groups[k][0]) + tt)
+                for f in range(2):
+                    nc.tensor.transpose(yb[:, tt, 128 * f:128 * (f + 1)], xtb[(k, f)][:, lo:lo + 128], ident_f[:])
+            ybank[n] = yb
+
+        def group_of(b, t):
+            if b == NB - 1 and t >= 8:
+                return (8, 12) if t < 12 else (12, 16)
+            return (0, 8) if t < 8 else (8, 16)
+
+        def rope(n):
+            b = n // UPB
+            t = 2 * (n % UPB)
+            g0, g1 = group_of(b, t)
+            if t == g0:
+                ystage[b] = ypool.tile([P, 4, g1 - g0, 64], F32, tag="ys", name="ys%d_%d" % (b, g0))
+            ys = ystage[b]
+            tl = t - g0
+            yb = ybank[n]
+            mu = mpool.tile([P, 2, 2, 3, 64], F32, tag="mu", name="mu_%d" % n)
+            nc.vector.tensor_tensor(
+                out=mu[:],
+                in0=yb[:, :, 0:192].rearrange("p t (h d) -> p t h d", h=3).unsqueeze(2).to_broadcast([P, 2, 2, 3, 64]),
+                in1=tab[:, t:t + 2].unsqueeze(3).to_broadcast([P, 2, 2, 3, 64]), op=MULT)
+            if V_COPY_ON_VECTOR:
+                nc.vector.tensor_copy(out=ys[:, 3, tl:tl + 2, :], in_=yb[:, :, 192:256])
+            else:
+                nc.scalar.copy(out=ys[:, 3, tl:tl + 2, :], in_=yb[:, :, 192:256])
+            eng = nc.vector if (TAIL_ON_VECTOR and n == NU - 1) else nc.gpsimd
+            eng.tensor_tensor(
+                out=ys[:, 0:3, tl:tl + 2, :].rearrange("p h t (i e) -> p t h i e", e=2),
+                in0=mu[:, :, 0].rearrange("p t h (i e) -> p t h i e", e=2),
+                in1=mu[:, :, 1].rearrange("p t h (i e) -> p t h i e", e=2)[:, :, :, :, ::-1], op=ADD)
+            if t + 2 == g1:
+                nc.sync.dma_start(out=out_0[b].rearrange("h (p t) d -> p h t d", t=TPP)[:, :, g0:g1, :],
+                                  in_=ys[:, 0:2, :, :])
+                nc.sync.dma_start(out=out_1[b, 0].rearrange("(p t) d -> p t d", t=TPP)[:, g0:g1, :],
+                                  in_=ys[:, 2, :, :])
+                nc.sync.dma_start(out=out_2[b, 0].rearrange("(p t) d -> p t d", t=TPP)[:, g0:g1, :],
+                                  in_=ys[:, 3, :, :])
+
+        transposes(0)
+        copies(0)
+        transposes(1)
+        quant(0)
+        mx(0)
+        copies(1)
+        evac(0)
+        for k in range(NG):
+            if k >= 1 and k + 2 < NG:
+                copies(k + 2)
+            if k + 1 < NG:
+                quant(k + 1)
+            for n in groups[k]:
+                back(n)
+            for n in groups[k]:
+                rope(n)
+            if k + 1 < NG:
+                mx(k + 1)
+                evac(k + 1)
+            if k == 0:
+                transposes(2)
+                copies(2)
+            if k + 3 < NG:
+                transposes(k + 3)

@@ -12,40 +12,34 @@ U8 = mybir.dt.uint8
 FP8X4 = mybir.dt.float8_e4m3fn_x4
 ADD = mybir.AluOpType.add
 MULT = mybir.AluOpType.mult
-IDENT = mybir.ActivationFunctionType.Identity
 
 P = 128
 NB = 4
 TPP = 16
 HID = 1024
-UPB = TPP // 2
-NU = NB * UPB
-
-MANUAL = True
-V_COPY_ON_VECTOR = True
-TAIL_ON_VECTOR = True
+STAGE = 8
+AHEAD = 5
 
 
 def tile_multiqueryattention_pa_t_kernel(tc, tensor, w_qkv, b_qkv, pos_emb, out_0, out_1, out_2):
     nc = tc.nc
     with ExitStack() as ctx:
         const = ctx.enter_context(tc.tile_pool(name="const", bufs=1))
-        xpool = ctx.enter_context(tc.tile_pool(name="xpool", bufs=1))
+        xpool = ctx.enter_context(tc.tile_pool(name="xpool", bufs=8))
         gpool = ctx.enter_context(tc.tile_pool(name="gpool", bufs=2))
         cpool = ctx.enter_context(tc.tile_pool(name="cpool", bufs=2))
-        epool = ctx.enter_context(tc.tile_pool(name="epool", bufs=2))
-        mpool = ctx.enter_context(tc.tile_pool(name="mpool", bufs=4))
+        mpool = ctx.enter_context(tc.tile_pool(name="mpool", bufs=2))
         ypool = ctx.enter_context(tc.tile_pool(name="ypool", bufs=3))
         psum = ctx.enter_context(tc.psum_pool(name="psum", bufs=1))
-        if MANUAL:
-            ctx.enter_context(tc.manual_schedule())
+        ctx.enter_context(tc.manual_schedule())
 
-        groups = [[0], [1]] + [[n, n + 1] for n in range(2, NU, 2)]
+        sizes = [2, 2] + [4] * 14 + [2, 2]
+        groups = []
+        first = 0
+        for s in sizes:
+            groups.append((first, s))
+            first += s
         NG = len(groups)
-        group_index = {}
-        for k in range(NG):
-            for n in groups[k]:
-                group_index[n] = k
 
         bb = const.tile([P, 256], BF16, name="bb")
         nc.scalar.dma_start(out=bb[:], in_=b_qkv.partition_broadcast(P))
@@ -53,52 +47,67 @@ def tile_multiqueryattention_pa_t_kernel(tc, tensor, w_qkv, b_qkv, pos_emb, out_
         nc.sync.dma_start(out=w_sb[:], in_=w_qkv.rearrange("(a p) k -> p a k", p=P))
         xsrc = {}
 
-        def load_x(n0, units):
-            b = n0 // UPB
-            t0 = 2 * (n0 % UPB)
+        def load_x(k):
+            n0, nt = groups[k]
+            b, t0 = divmod(n0, TPP)
             view = tensor[b].rearrange("(p t) k -> p t k", t=TPP)
-            xt = xpool.tile([P, 2 * units, HID], BF16, name="x%d" % n0)
-            nc.sync.dma_start(out=xt[:], in_=view[:, t0:t0 + 2 * units, :])
-            for j in range(2 * units):
-                xsrc[(n0 + j // 2, j % 2)] = xt[:, j, :]
+            xt = xpool.tile([P, nt, HID], BF16, tag="x", name="x%d" % k)
+            nc.sync.dma_start(out=xt[:], in_=view[:, t0:t0 + nt, :])
+            xsrc[k] = xt
 
-        load_x(0, 1)
-        load_x(1, 1)
         pe_sb = const.tile([P, TPP, 128], BF16, name="pe_sb")
+        load_x(0)
         nc.sync.dma_start(out=pe_sb[:], in_=pos_emb.rearrange("(p t) c -> p t c", t=TPP))
-        for n0 in range(2, NU, 2):
-            load_x(n0, 2)
+        for k in range(1, AHEAD):
+            load_x(k)
 
         ident_f = const.tile([P, P], F32, name="ident_f")
         make_identity(nc, ident_f[:])
+        ident_b = const.tile([P, P], BF16, name="ident_b")
+        nc.vector.tensor_copy(out=ident_b[:], in_=ident_f[:])
+        flip_f = const.tile([P, P], F32, name="flip_f")
+        nc.vector.tensor_copy(out=flip_f[:].rearrange("p (i e) -> p i e", e=2),
+                              in_=ident_f[:].rearrange("p (i e) -> p i e", e=2)[:, :, ::-1])
 
-        bsel = const.tile([P, 2, P], F32, name="bsel")
-        nc.vector.tensor_tensor(
-            out=bsel[:], in0=bb[:].rearrange("p (f j) -> p f j", f=2),
-            in1=ident_f[:].unsqueeze(1).to_broadcast([P, 2, P]), op=MULT)
-        bcol = const.tile([P, 2], F32, name="bcol")
+        bsel = const.tile([P, P], F32, name="bsel")
+        nc.vector.tensor_tensor(out=bsel[:], in0=bb[:, 0:P], in1=ident_f[:], op=MULT)
+        bcol = const.tile([P, 1], F32, name="bcol")
         nc.vector.tensor_reduce(out=bcol[:], in_=bsel[:], axis=mybir.AxisListType.X, op=ADD)
 
-        tab = const.tile([P, TPP, 2, 64], BF16, name="tab")
+        tab = const.tile([P, TPP, 2, 2, 64], BF16, name="tab")
+        tabt = const.tile([P, 2, TPP * P], BF16, name="tabt")
 
-        def build_tab(ta0, ta1):
-            cos_src = pe_sb[:, ta0:ta1, 0:64]
-            sin_src = pe_sb[:, ta0:ta1, 64:128].rearrange("p t (i e) -> p t i e", e=2)[:, :, :, ::-1]
-            sin_dst = tab[:, ta0:ta1, 1, :].rearrange("p t (i e) -> p t i e", e=2)
-            nc.gpsimd.tensor_scalar(out=tab[:, ta0:ta1, 0, :], in0=cos_src, scalar1=1.0, scalar2=0.0,
-                                    op0=MULT, op1=ADD)
-            nc.gpsimd.tensor_scalar(out=sin_dst, in0=sin_src, scalar1=1.0, scalar2=0.0, op0=MULT, op1=ADD)
+        def build_tab(q):
+            ta, tb = 4 * q, 4 * q + 4
+            nc.gpsimd.tensor_scalar(out=tab[:, ta:tb, 0, :, :],
+                                    in0=pe_sb[:, ta:tb, 0:64].unsqueeze(2).to_broadcast([P, 4, 2, 64]),
+                                    scalar1=1.0, scalar2=0.0, op0=MULT, op1=ADD)
+            for h in range(2):
+                nc.gpsimd.tensor_scalar(
+                    out=tab[:, ta:tb, 1, h, :].rearrange("p t (i e) -> p t i e", e=2),
+                    in0=pe_sb[:, ta:tb, 64:128].rearrange("p t (i e) -> p t i e", e=2)[:, :, :, ::-1],
+                    scalar1=1.0, scalar2=0.0, op0=MULT, op1=ADD)
 
-        build_tab(0, 4)
-        build_tab(4, TPP)
+        def turn_tab(q):
+            xb = psum.tile([P, 2, 4, P], BF16, tag="X", name="X%d" % q)
+            for c in range(2):
+                for i in range(4):
+                    nc.tensor.transpose(xb[:, c, i, :], tab[:, 4 * q + i, c, :, :].rearrange("p h d -> p (h d)"),
+                                        ident_b[:])
+            nc.scalar.copy(out=tabt[:, :, 512 * q:512 * (q + 1)], in_=xb[:].rearrange("p c i r -> p c (i r)"))
+
+        for q in range(4):
+            build_tab(q)
 
         wg = const.tile([P, 2048], BF16, name="wg", align_bytes=64)
         wg_f = wg[:].bitcast(F32).rearrange("p (g n u) -> p g n u", g=2, u=2)
         for a in range(2):
             tw = psum.tile([P, 512], F32, tag="T%d" % (2 + a), name="tw%d" % a)
             wa = w_sb[:, a, :].bitcast(F32)
-            for q in range(4):
-                nc.tensor.transpose(tw[:, 128 * q:128 * (q + 1)], wa[:, 256 * (q // 2) + q % 2:256 * (q // 2 + 1):2], ident_f[:])
+            for g in range(2):
+                for u in range(2):
+                    nc.tensor.transpose(tw[:, 256 * g + 128 * u:256 * g + 128 * (u + 1)],
+                                        wa[:, 256 * g + u:256 * (g + 1):2], ident_f[:])
             src = tw[:].rearrange("p (g u n) -> p g n u", g=2, u=2)
             if a == 0:
                 nc.scalar.copy(out=wg_f[:, :, 0:128, :], in_=src)
@@ -108,128 +117,139 @@ def tile_multiqueryattention_pa_t_kernel(tc, tensor, w_qkv, b_qkv, pos_emb, out_
         ws = const.tile([P, 512], U8, name="ws", align_bytes=64)
         nc.vector.quantize_mx(out=wc[:].bitcast(FP8X4), scales=ws[:], in_=wg[:])
 
-        tbank = {}
-        grp = {}
-        codes = {}
-        fbank = {}
-        xtb = {}
-        ybank = {}
-        work = {}
-        ystage = {}
+        tbank, grp, codes, qbank, kvbank, mqs, stage = {}, {}, {}, {}, {}, {}, {}
 
         def transposes(k):
-            for n in groups[k]:
-                for tt in range(2):
-                    tp = psum.tile([P, 512], F32, tag="T%d" % ((2 * n + tt) % 4), name="T%d_%d" % (tt, n))
-                    xa = xsrc[(n, tt)].bitcast(F32)
-                    for q in range(4):
-                        nc.tensor.transpose(tp[:, 128 * q:128 * (q + 1)], xa[:, 256 * (q // 2) + q % 2:256 * (q // 2 + 1):2], ident_f[:])
-                    tbank[(n, tt)] = tp
+            n0, nt = groups[k]
+            for i in range(nt):
+                tp = psum.tile([P, 512], F32, tag="T%d" % ((n0 + i) % 4), name="T_%d" % (n0 + i))
+                xa = xsrc[k][:, i, :].bitcast(F32)
+                for g in range(2):
+                    for u in range(2):
+                        nc.tensor.transpose(tp[:, 256 * g + 128 * u:256 * g + 128 * (u + 1)],
+                                            xa[:, 256 * g + u:256 * (g + 1):2], ident_f[:])
+                tbank[(k, i)] = tp
 
         def copies(k):
-            tiles = 2 * len(groups[k])
-            g = gpool.tile([P, tiles * HID], BF16, tag="grp", name="grp%d" % k, align_bytes=64)
-            gf = g[:].bitcast(F32).rearrange("p (g i r u) -> p g i r u", g=2, i=tiles, u=2)
-            for n in groups[k]:
-                for tt in range(2):
-                    nc.scalar.copy(out=gf[:, :, 2 * (n - groups[k][0]) + tt],
-                                   in_=tbank[(n, tt)][:].rearrange("p (g u r) -> p g r u", g=2, u=2))
-            grp[k] = g
+            n0, nt = groups[k]
+            gt = gpool.tile([P, nt * HID], BF16, tag="grp", name="grp%d" % k, align_bytes=64)
+            gf = gt[:].bitcast(F32).rearrange("p (g i r u) -> p g i r u", g=2, i=nt, u=2)
+            for i in range(nt):
+                nc.scalar.copy(out=gf[:, :, i], in_=tbank[(k, i)][:].rearrange("p (g u r) -> p g r u", g=2, u=2))
+            grp[k] = gt
 
         def quant(k):
-            tiles = 2 * len(groups[k])
-            c = cpool.tile([P, tiles * 256], U32, tag="codes", name="codes%d" % k, align_bytes=64)
-            s = cpool.tile([P, tiles * 256], U8, tag="scl", name="scl%d" % k, align_bytes=64)
+            n0, nt = groups[k]
+            c = cpool.tile([P, nt * 256], U32, tag="codes", name="codes%d" % k, align_bytes=64)
+            s = cpool.tile([P, nt * 256], U8, tag="scl", name="scl%d" % k, align_bytes=64)
             nc.vector.quantize_mx(out=c[:].bitcast(FP8X4), scales=s[:], in_=grp[k][:])
             codes[k] = (c, s)
 
         def mx(k):
+            n0, nt = groups[k]
             c, s = codes[k]
-            ntok = 256 * len(groups[k])
-            for f in range(2):
-                fb = psum.tile([P, ntok], F32, tag="F%d" % f, name="F%d_%d" % (f, k))
+            w = nt * P
+            qb = psum.tile([P, w], F32, tag="Q", name="Q%d" % k)
+            for g in range(2):
+                nc.tensor.matmul_mx(
+                    out=qb[:],
+                    lhsT=wc[:, 256 * g:256 * g + 128].bitcast(FP8X4), lhsT_scale=ws[:, 256 * g:256 * g + 128],
+                    rhs=c[:, w * g:w * (g + 1)].bitcast(FP8X4), rhs_scale=s[:, w * g:w * (g + 1)],
+                    start=(g == 0), stop=(g == 1))
+            qbank[k] = qb
+            kvb = psum.tile([P, nt, P], F32, tag="KV", name="KV%d" % k)
+            for i in range(nt):
                 for g in range(2):
-                    lo = 256 * g + 128 * f
+                    lo = w * g + P * i
                     nc.tensor.matmul_mx(
-                        out=fb[:],
-                        lhsT=wc[:, lo:lo + 128].bitcast(FP8X4), lhsT_scale=ws[:, lo:lo + 128],
-                        rhs=c[:, ntok * g:ntok * (g + 1)].bitcast(FP8X4), rhs_scale=s[:, ntok * g:ntok * (g + 1)],
+                        out=kvb[:, i, :],
+                        lhsT=c[:, lo:lo + P].bitcast(FP8X4), lhsT_scale=s[:, lo:lo + P],
+                        rhs=wc[:, 256 * g + 128:256 * (g + 1)].bitcast(FP8X4),
+                        rhs_scale=ws[:, 256 * g + 128:256 * (g + 1)],
                         start=(g == 0), stop=(g == 1))
-                fbank[(k, f)] = fb
+            kvbank[k] = kvb
 
-        def evac(k):
-            ntok = 256 * len(groups[k])
-            for f in range(2):
-                xt = epool.tile([P, ntok], F32, tag="xtb%d" % f, name="xtb%d_%d" % (f, k))
-                nc.scalar.activation(out=xt[:], in_=fbank[(k, f)][:], func=IDENT, bias=bcol[:, f:f + 1], scale=1.0)
-                xtb[(k, f)] = xt
+        def rope_q(k):
+            n0, nt = groups[k]
+            t = n0 % TPP
+            mq = mpool.tile([P, 2, nt * P], F32, tag="mq", name="mq%d" % k)
+            for c in range(2):
+                nc.vector.scalar_tensor_tensor(out=mq[:, c, :], in0=qbank[k][:], scalar=bcol[:, 0:1],
+                                               in1=tabt[:, c, P * t:P * (t + nt)], op0=ADD, op1=MULT)
+            mqs[k] = mq
 
-        def back(n):
-            k = group_index[n]
-            yb = psum.tile([P, 2, 256], F32, tag="Y%d" % (n % 2), name="Y_%d" % n)
-            for tt in range(2):
-                lo = 128 * (2 * (n - groups[k][0]) + tt)
-                for f in range(2):
-                    nc.tensor.transpose(yb[:, tt, 128 * f:128 * (f + 1)], xtb[(k, f)][:, lo:lo + 128], ident_f[:])
-            ybank[n] = yb
+        def stage_of(k):
+            n0, nt = groups[k]
+            s = n0 // STAGE
+            if s not in stage:
+                kvs = ypool.tile([P, 2, STAGE, 64], F32, tag="kvs", name="kvs%d" % s)
+                ysk = ypool.tile([P, STAGE, 64], F32, tag="ysk", name="ysk%d" % s)
+                ysq = ypool.tile([P, 2, STAGE, 64], F32, tag="ysq", name="ysq%d" % s)
+                stage[s] = (kvs, ysk, ysq)
+            return stage[s]
 
-        def group_of(b, t):
-            if b == NB - 1 and t >= 8:
-                return (8, 12) if t < 12 else (12, 16)
-            return (0, 8) if t < 8 else (8, 16)
-
-        def rope(n):
-            b = n // UPB
-            t = 2 * (n % UPB)
-            g0, g1 = group_of(b, t)
-            if t == g0:
-                ystage[b] = ypool.tile([P, 4, g1 - g0, 64], F32, tag="ys", name="ys%d_%d" % (b, g0))
-            ys = ystage[b]
-            tl = t - g0
-            yb = ybank[n]
-            mu = mpool.tile([P, 2, 2, 3, 64], F32, tag="mu", name="mu_%d" % n)
+        def kv(k):
+            n0, nt = groups[k]
+            t = n0 % TPP
+            tl = n0 % STAGE
+            kvs, ysk, ysq = stage_of(k)
             nc.vector.tensor_tensor(
-                out=mu[:],
-                in0=yb[:, :, 0:192].rearrange("p t (h d) -> p t h d", h=3).unsqueeze(2).to_broadcast([P, 2, 2, 3, 64]),
-                in1=tab[:, t:t + 2].unsqueeze(3).to_broadcast([P, 2, 2, 3, 64]), op=MULT)
-            if V_COPY_ON_VECTOR:
-                nc.vector.tensor_copy(out=ys[:, 3, tl:tl + 2, :], in_=yb[:, :, 192:256])
-            else:
-                nc.scalar.copy(out=ys[:, 3, tl:tl + 2, :], in_=yb[:, :, 192:256])
-            eng = nc.vector if (TAIL_ON_VECTOR and n == NU - 1) else nc.gpsimd
-            eng.tensor_tensor(
-                out=ys[:, 0:3, tl:tl + 2, :].rearrange("p h t (i e) -> p t h i e", e=2),
-                in0=mu[:, :, 0].rearrange("p t h (i e) -> p t h i e", e=2),
-                in1=mu[:, :, 1].rearrange("p t h (i e) -> p t h i e", e=2)[:, :, :, :, ::-1], op=ADD)
-            if t + 2 == g1:
-                nc.sync.dma_start(out=out_0[b].rearrange("h (p t) d -> p h t d", t=TPP)[:, :, g0:g1, :],
-                                  in_=ys[:, 0:2, :, :])
-                nc.sync.dma_start(out=out_1[b, 0].rearrange("(p t) d -> p t d", t=TPP)[:, g0:g1, :],
-                                  in_=ys[:, 2, :, :])
-                nc.sync.dma_start(out=out_2[b, 0].rearrange("(p t) d -> p t d", t=TPP)[:, g0:g1, :],
-                                  in_=ys[:, 3, :, :])
+                out=kvs[:, :, tl:tl + nt, :].rearrange("p h t d -> p t h d"),
+                in0=kvbank[k][:].rearrange("p t (h d) -> p t h d", h=2),
+                in1=bb[:, 128:256].rearrange("p (h d) -> p h d", h=2).unsqueeze(1).to_broadcast([P, nt, 2, 64]),
+                op=ADD)
+            mk = mpool.tile([P, nt, 2, 64], F32, tag="mk", name="mk%d" % k)
+            nc.vector.tensor_tensor(
+                out=mk[:], in0=kvs[:, 0, tl:tl + nt, :].unsqueeze(2).to_broadcast([P, nt, 2, 64]),
+                in1=tab[:, t:t + nt, :, 0, :], op=MULT)
+            nc.gpsimd.tensor_tensor(
+                out=ysk[:, tl:tl + nt, :].rearrange("p t (i e) -> p t i e", e=2),
+                in0=mk[:, :, 0].rearrange("p t (i e) -> p t i e", e=2),
+                in1=mk[:, :, 1].rearrange("p t (i e) -> p t i e", e=2)[:, :, :, ::-1], op=ADD)
+
+        def back(k):
+            n0, nt = groups[k]
+            tl = n0 % STAGE
+            s = n0 // STAGE
+            kvs, ysk, ysq = stage_of(k)
+            yb = psum.tile([P, nt, P], F32, tag="Y", name="Y%d" % k)
+            for i in range(nt):
+                for c in range(2):
+                    nc.tensor.matmul(out=yb[:, i, :], lhsT=mqs[k][:, c, P * i:P * (i + 1)],
+                                     rhs=(ident_f if c == 0 else flip_f)[:], is_transpose=True,
+                                     start=(c == 0), stop=(c == 1))
+            nc.scalar.copy(out=ysq[:, :, tl:tl + nt, :].rearrange("p h t d -> p t h d"),
+                           in_=yb[:].rearrange("p t (h d) -> p t h d", h=2))
+            if tl + nt == STAGE:
+                b, t0 = divmod(s * STAGE, TPP)
+                t1 = t0 + STAGE
+                nc.sync.dma_start(out=out_2[b, 0].rearrange("(p t) d -> p t d", t=TPP)[:, t0:t1, :],
+                                  in_=kvs[:, 1, :, :])
+                nc.sync.dma_start(out=out_1[b, 0].rearrange("(p t) d -> p t d", t=TPP)[:, t0:t1, :],
+                                  in_=ysk[:])
+                nc.sync.dma_start(out=out_0[b].rearrange("h (p t) d -> p h t d", t=TPP)[:, :, t0:t1, :],
+                                  in_=ysq[:])
 
         transposes(0)
         copies(0)
+        turn_tab(0)
         transposes(1)
         quant(0)
-        mx(0)
         copies(1)
-        evac(0)
         for k in range(NG):
-            if k >= 1 and k + 2 < NG:
-                copies(k + 2)
+            mx(k)
+            if k >= 1:
+                back(k - 1)
+            if k in (1, 2, 3):
+                turn_tab(k)
+            if k + 2 < NG:
+                transposes(k + 2)
             if k + 1 < NG:
                 quant(k + 1)
-            for n in groups[k]:
-                back(n)
-            for n in groups[k]:
-                rope(n)
-            if k + 1 < NG:
-                mx(k + 1)
-                evac(k + 1)
-            if k == 0:
-                transposes(2)
-                copies(2)
-            if k + 3 < NG:
-                transposes(k + 3)
+            rope_q(k)
+            kv(k)
+            if k + 2 < NG:
+                copies(k + 2)
+            if k + AHEAD < NG:
+                load_x(k + AHEAD)
+        back(NG - 1)

@@ -12,153 +12,136 @@ U8 = mybir.dt.uint8
 FP8X4 = mybir.dt.float8_e4m3fn_x4
 ADD = mybir.AluOpType.add
 MULT = mybir.AluOpType.mult
+IDENT = mybir.ActivationFunctionType.Identity
 
 P = 128
 NB = 4
 TPP = 16
 HID = 1024
+NT = 2
+NU = NB * TPP // NT
 STAGE = 8
-AHEAD = 5
+AHEAD = 8
 
 
 def tile_multiqueryattention_pa_t_kernel(tc, tensor, w_qkv, b_qkv, pos_emb, out_0, out_1, out_2):
     nc = tc.nc
     with ExitStack() as ctx:
         const = ctx.enter_context(tc.tile_pool(name="const", bufs=1))
-        xpool = ctx.enter_context(tc.tile_pool(name="xpool", bufs=8))
-        gpool = ctx.enter_context(tc.tile_pool(name="gpool", bufs=2))
+        xpool = ctx.enter_context(tc.tile_pool(name="xpool", bufs=12))
+        gpool = ctx.enter_context(tc.tile_pool(name="gpool", bufs=3))
         cpool = ctx.enter_context(tc.tile_pool(name="cpool", bufs=2))
-        mpool = ctx.enter_context(tc.tile_pool(name="mpool", bufs=2))
+        mpool = ctx.enter_context(tc.tile_pool(name="mpool", bufs=3))
         ypool = ctx.enter_context(tc.tile_pool(name="ypool", bufs=3))
         psum = ctx.enter_context(tc.psum_pool(name="psum", bufs=1))
         ctx.enter_context(tc.manual_schedule())
 
-        sizes = [2, 2] + [4] * 14 + [2, 2]
-        groups = []
-        first = 0
-        for s in sizes:
-            groups.append((first, s))
-            first += s
-        NG = len(groups)
-
         bb = const.tile([P, 256], BF16, name="bb")
         nc.scalar.dma_start(out=bb[:], in_=b_qkv.partition_broadcast(P))
-        w_sb = const.tile([P, 2, HID], BF16, name="w_sb")
-        nc.sync.dma_start(out=w_sb[:], in_=w_qkv.rearrange("(a p) k -> p a k", p=P))
         xsrc = {}
 
-        def load_x(k):
-            n0, nt = groups[k]
-            b, t0 = divmod(n0, TPP)
+        def load_x(u):
+            b, t0 = divmod(u * NT, TPP)
             view = tensor[b].rearrange("(p t) k -> p t k", t=TPP)
-            xt = xpool.tile([P, nt, HID], BF16, tag="x", name="x%d" % k)
-            nc.sync.dma_start(out=xt[:], in_=view[:, t0:t0 + nt, :])
-            xsrc[k] = xt
+            xt = xpool.tile([P, NT, HID], BF16, tag="x", name="x%d" % u)
+            nc.sync.dma_start(out=xt[:], in_=view[:, t0:t0 + NT, :])
+            xsrc[u] = xt
 
-        pe_sb = const.tile([P, TPP, 128], BF16, name="pe_sb")
         load_x(0)
+        w_sb = const.tile([P, 2, HID], BF16, name="w_sb")
+        nc.sync.dma_start(out=w_sb[:], in_=w_qkv.rearrange("(a p) k -> p a k", p=P))
+        load_x(1)
+        pe_sb = const.tile([P, TPP, 128], BF16, name="pe_sb")
         nc.sync.dma_start(out=pe_sb[:], in_=pos_emb.rearrange("(p t) c -> p t c", t=TPP))
-        for k in range(1, AHEAD):
-            load_x(k)
+        for u in range(2, AHEAD):
+            load_x(u)
 
+        warm = const.tile([P, 2], F32, name="warm")
+        nc.vector.memset(warm[:], 0.0)
+        nc.scalar.activation(out=warm[:, 0:1], in_=warm[:, 1:2], func=IDENT, bias=0.0, scale=1.0)
         ident_f = const.tile([P, P], F32, name="ident_f")
         make_identity(nc, ident_f[:])
-        ident_b = const.tile([P, P], BF16, name="ident_b")
-        nc.vector.tensor_copy(out=ident_b[:], in_=ident_f[:])
-        flip_f = const.tile([P, P], F32, name="flip_f")
-        nc.vector.tensor_copy(out=flip_f[:].rearrange("p (i e) -> p i e", e=2),
-                              in_=ident_f[:].rearrange("p (i e) -> p i e", e=2)[:, :, ::-1])
 
         bsel = const.tile([P, P], F32, name="bsel")
         nc.vector.tensor_tensor(out=bsel[:], in0=bb[:, 0:P], in1=ident_f[:], op=MULT)
         bcol = const.tile([P, 1], F32, name="bcol")
         nc.vector.tensor_reduce(out=bcol[:], in_=bsel[:], axis=mybir.AxisListType.X, op=ADD)
 
-        tab = const.tile([P, TPP, 2, 2, 64], BF16, name="tab")
-        tabt = const.tile([P, 2, TPP * P], BF16, name="tabt")
+        tab = const.tile([P, TPP, 2, 64], BF16, name="tab")
 
-        def build_tab(q):
-            ta, tb = 4 * q, 4 * q + 4
-            nc.gpsimd.tensor_scalar(out=tab[:, ta:tb, 0, :, :],
-                                    in0=pe_sb[:, ta:tb, 0:64].unsqueeze(2).to_broadcast([P, 4, 2, 64]),
+        def build_tab(ta, tb):
+            nc.gpsimd.tensor_scalar(out=tab[:, ta:tb, 0, :], in0=pe_sb[:, ta:tb, 0:64],
                                     scalar1=1.0, scalar2=0.0, op0=MULT, op1=ADD)
-            for h in range(2):
-                nc.gpsimd.tensor_scalar(
-                    out=tab[:, ta:tb, 1, h, :].rearrange("p t (i e) -> p t i e", e=2),
-                    in0=pe_sb[:, ta:tb, 64:128].rearrange("p t (i e) -> p t i e", e=2)[:, :, :, ::-1],
-                    scalar1=1.0, scalar2=0.0, op0=MULT, op1=ADD)
+            nc.gpsimd.tensor_scalar(
+                out=tab[:, ta:tb, 1, :].rearrange("p t (i e) -> p t i e", e=2),
+                in0=pe_sb[:, ta:tb, 64:128].rearrange("p t (i e) -> p t i e", e=2)[:, :, :, ::-1],
+                scalar1=1.0, scalar2=0.0, op0=MULT, op1=ADD)
 
-        def turn_tab(q):
-            xb = psum.tile([P, 2, 4, P], BF16, tag="X", name="X%d" % q)
-            for c in range(2):
-                for i in range(4):
-                    nc.tensor.transpose(xb[:, c, i, :], tab[:, 4 * q + i, c, :, :].rearrange("p h d -> p (h d)"),
-                                        ident_b[:])
-            nc.scalar.copy(out=tabt[:, :, 512 * q:512 * (q + 1)], in_=xb[:].rearrange("p c i r -> p c (i r)"))
-
-        for q in range(4):
-            build_tab(q)
+        build_tab(0, 4)
+        build_tab(4, TPP)
 
         wg = const.tile([P, 2048], BF16, name="wg", align_bytes=64)
-        wg_f = wg[:].bitcast(F32).rearrange("p (g n u) -> p g n u", g=2, u=2)
-        for a in range(2):
-            tw = psum.tile([P, 512], F32, tag="T%d" % (2 + a), name="tw%d" % a)
-            wa = w_sb[:, a, :].bitcast(F32)
-            for g in range(2):
-                for u in range(2):
-                    nc.tensor.transpose(tw[:, 256 * g + 128 * u:256 * g + 128 * (u + 1)],
-                                        wa[:, 256 * g + u:256 * (g + 1):2], ident_f[:])
-            src = tw[:].rearrange("p (g u n) -> p g n u", g=2, u=2)
-            if a == 0:
-                nc.scalar.copy(out=wg_f[:, :, 0:128, :], in_=src)
-            else:
-                nc.vector.tensor_copy(out=wg_f[:, :, 128:256, :], in_=src)
         wc = const.tile([P, 512], U32, name="wc", align_bytes=64)
         ws = const.tile([P, 512], U8, name="ws", align_bytes=64)
-        nc.vector.quantize_mx(out=wc[:].bitcast(FP8X4), scales=ws[:], in_=wg[:])
 
-        tbank, grp, codes, qbank, kvbank, mqs, stage = {}, {}, {}, {}, {}, {}, {}
-
-        def transposes(k):
-            n0, nt = groups[k]
-            for i in range(nt):
-                tp = psum.tile([P, 512], F32, tag="T%d" % ((n0 + i) % 4), name="T_%d" % (n0 + i))
-                xa = xsrc[k][:, i, :].bitcast(F32)
+        def weights():
+            wg_f = wg[:].bitcast(F32).rearrange("p (g n u) -> p g n u", g=2, u=2)
+            for a in range(2):
+                tw = psum.tile([P, 512], F32, tag="T%d" % (2 + a), name="tw%d" % a)
+                wa = w_sb[:, a, :].bitcast(F32)
                 for g in range(2):
                     for u in range(2):
-                        nc.tensor.transpose(tp[:, 256 * g + 128 * u:256 * g + 128 * (u + 1)],
-                                            xa[:, 256 * g + u:256 * (g + 1):2], ident_f[:])
-                tbank[(k, i)] = tp
+                        nc.tensor.transpose(tw[:, 256 * g + 128 * u:256 * g + 128 * (u + 1)],
+                                            wa[:, 256 * g + u:256 * (g + 1):2], ident_f[:])
+                src = tw[:].rearrange("p (g u n) -> p g n u", g=2, u=2)
+                if a == 0:
+                    nc.scalar.copy(out=wg_f[:, :, 0:128, :], in_=src)
+                else:
+                    nc.vector.tensor_copy(out=wg_f[:, :, 128:256, :], in_=src)
+            nc.vector.quantize_mx(out=wc[:].bitcast(FP8X4), scales=ws[:], in_=wg[:])
 
-        def copies(k):
-            n0, nt = groups[k]
-            gt = gpool.tile([P, nt * HID], BF16, tag="grp", name="grp%d" % k, align_bytes=64)
-            gf = gt[:].bitcast(F32).rearrange("p (g i r u) -> p g i r u", g=2, i=nt, u=2)
-            for i in range(nt):
-                nc.scalar.copy(out=gf[:, :, i], in_=tbank[(k, i)][:].rearrange("p (g u r) -> p g r u", g=2, u=2))
-            grp[k] = gt
+        tbank, grp, codes, qbank, kvbank, xqs, ybank, mus, stage, pres = {}, {}, {}, {}, {}, {}, {}, {}, {}, {}
 
-        def quant(k):
-            n0, nt = groups[k]
-            c = cpool.tile([P, nt * 256], U32, tag="codes", name="codes%d" % k, align_bytes=64)
-            s = cpool.tile([P, nt * 256], U8, tag="scl", name="scl%d" % k, align_bytes=64)
-            nc.vector.quantize_mx(out=c[:].bitcast(FP8X4), scales=s[:], in_=grp[k][:])
-            codes[k] = (c, s)
+        def transposes(u):
+            for i in range(NT):
+                tp = psum.tile([P, 512], F32, tag="T%d" % ((NT * u + i) % 4), name="T%d_%d" % (u, i))
+                xa = xsrc[u][:, i, :].bitcast(F32)
+                for g in range(2):
+                    for h in range(2):
+                        nc.tensor.transpose(tp[:, 256 * g + 128 * h:256 * g + 128 * (h + 1)],
+                                            xa[:, 256 * g + h:256 * (g + 1):2], ident_f[:])
+                tbank[(u, i)] = tp
 
-        def mx(k):
-            n0, nt = groups[k]
-            c, s = codes[k]
-            w = nt * P
-            qb = psum.tile([P, w], F32, tag="Q", name="Q%d" % k)
+        def copies(u):
+            gt = gpool.tile([P, NT * HID], BF16, tag="grp", name="grp%d" % u, align_bytes=64)
+            gf = gt[:].bitcast(F32).rearrange("p (g i r h) -> p g i r h", g=2, i=NT, h=2)
+            for i in range(NT):
+                nc.scalar.copy(out=gf[:, :, i], in_=tbank[(u, i)][:].rearrange("p (g h r) -> p g r h", g=2, h=2))
+            grp[u] = gt
+
+        def quant(u):
+            c = cpool.tile([P, NT * 256], U32, tag="codes", name="codes%d" % u, align_bytes=64)
+            s = cpool.tile([P, NT * 256], U8, tag="scl", name="scl%d" % u, align_bytes=64)
+            nc.vector.quantize_mx(out=c[:].bitcast(FP8X4), scales=s[:], in_=grp[u][:])
+            codes[u] = (c, s)
+
+        def mx_q(u):
+            c, s = codes[u]
+            w = NT * P
+            qb = psum.tile([P, w], F32, tag="Q", name="Q%d" % u)
             for g in range(2):
                 nc.tensor.matmul_mx(
                     out=qb[:],
                     lhsT=wc[:, 256 * g:256 * g + 128].bitcast(FP8X4), lhsT_scale=ws[:, 256 * g:256 * g + 128],
                     rhs=c[:, w * g:w * (g + 1)].bitcast(FP8X4), rhs_scale=s[:, w * g:w * (g + 1)],
                     start=(g == 0), stop=(g == 1))
-            qbank[k] = qb
-            kvb = psum.tile([P, nt, P], F32, tag="KV", name="KV%d" % k)
-            for i in range(nt):
+            qbank[u] = qb
+
+        def mx_kv(u):
+            c, s = codes[u]
+            w = NT * P
+            kvb = psum.tile([P, NT, P], F32, tag="KV%d" % (u % 2), name="KV_%d" % u)
+            for i in range(NT):
                 for g in range(2):
                     lo = w * g + P * i
                     nc.tensor.matmul_mx(
@@ -167,89 +150,83 @@ def tile_multiqueryattention_pa_t_kernel(tc, tensor, w_qkv, b_qkv, pos_emb, out_
                         rhs=wc[:, 256 * g + 128:256 * (g + 1)].bitcast(FP8X4),
                         rhs_scale=ws[:, 256 * g + 128:256 * (g + 1)],
                         start=(g == 0), stop=(g == 1))
-            kvbank[k] = kvb
+            kvbank[u] = kvb
 
-        def rope_q(k):
-            n0, nt = groups[k]
-            t = n0 % TPP
-            mq = mpool.tile([P, 2, nt * P], F32, tag="mq", name="mq%d" % k)
-            for c in range(2):
-                nc.vector.scalar_tensor_tensor(out=mq[:, c, :], in0=qbank[k][:], scalar=bcol[:, 0:1],
-                                               in1=tabt[:, c, P * t:P * (t + nt)], op0=ADD, op1=MULT)
-            mqs[k] = mq
+        def bias_q(u):
+            xq = mpool.tile([P, NT * P], F32, tag="xq", name="xq%d" % u)
+            nc.scalar.activation(out=xq[:], in_=qbank[u][:], func=IDENT, bias=bcol[:, 0:1], scale=1.0)
+            xqs[u] = xq
 
-        def stage_of(k):
-            n0, nt = groups[k]
-            s = n0 // STAGE
+        def back(u):
+            yb = psum.tile([P, NT, P], F32, tag="Y", name="Y%d" % u)
+            for i in range(NT):
+                nc.tensor.transpose(yb[:, i, :], xqs[u][:, P * i:P * (i + 1)], ident_f[:])
+            ybank[u] = yb
+
+        def stage_of(u):
+            s = NT * u // STAGE
             if s not in stage:
                 kvs = ypool.tile([P, 2, STAGE, 64], F32, tag="kvs", name="kvs%d" % s)
-                ysk = ypool.tile([P, STAGE, 64], F32, tag="ysk", name="ysk%d" % s)
-                ysq = ypool.tile([P, 2, STAGE, 64], F32, tag="ysq", name="ysq%d" % s)
-                stage[s] = (kvs, ysk, ysq)
+                ys = ypool.tile([P, 3, STAGE, 64], F32, tag="ys", name="ys%d" % s)
+                stage[s] = (kvs, ys)
             return stage[s]
 
-        def kv(k):
-            n0, nt = groups[k]
-            t = n0 % TPP
-            tl = n0 % STAGE
-            kvs, ysk, ysq = stage_of(k)
+        def bias_kv(u):
+            tl = NT * u % STAGE
+            kvs, ys = stage_of(u)
             nc.vector.tensor_tensor(
-                out=kvs[:, :, tl:tl + nt, :].rearrange("p h t d -> p t h d"),
-                in0=kvbank[k][:].rearrange("p t (h d) -> p t h d", h=2),
-                in1=bb[:, 128:256].rearrange("p (h d) -> p h d", h=2).unsqueeze(1).to_broadcast([P, nt, 2, 64]),
+                out=kvs[:, :, tl:tl + NT, :].rearrange("p h t d -> p t h d"),
+                in0=kvbank[u][:].rearrange("p t (h d) -> p t h d", h=2),
+                in1=bb[:, 128:256].rearrange("p (h d) -> p h d", h=2).unsqueeze(1).to_broadcast([P, NT, 2, 64]),
                 op=ADD)
-            mk = mpool.tile([P, nt, 2, 64], F32, tag="mk", name="mk%d" % k)
-            nc.vector.tensor_tensor(
-                out=mk[:], in0=kvs[:, 0, tl:tl + nt, :].unsqueeze(2).to_broadcast([P, nt, 2, 64]),
-                in1=tab[:, t:t + nt, :, 0, :], op=MULT)
-            nc.gpsimd.tensor_tensor(
-                out=ysk[:, tl:tl + nt, :].rearrange("p t (i e) -> p t i e", e=2),
-                in0=mk[:, :, 0].rearrange("p t (i e) -> p t i e", e=2),
-                in1=mk[:, :, 1].rearrange("p t (i e) -> p t i e", e=2)[:, :, :, ::-1], op=ADD)
 
-        def back(k):
-            n0, nt = groups[k]
-            tl = n0 % STAGE
-            s = n0 // STAGE
-            kvs, ysk, ysq = stage_of(k)
-            yb = psum.tile([P, nt, P], F32, tag="Y", name="Y%d" % k)
-            for i in range(nt):
-                for c in range(2):
-                    nc.tensor.matmul(out=yb[:, i, :], lhsT=mqs[k][:, c, P * i:P * (i + 1)],
-                                     rhs=(ident_f if c == 0 else flip_f)[:], is_transpose=True,
-                                     start=(c == 0), stop=(c == 1))
-            nc.scalar.copy(out=ysq[:, :, tl:tl + nt, :].rearrange("p h t d -> p t h d"),
-                           in_=yb[:].rearrange("p t (h d) -> p t h d", h=2))
-            if tl + nt == STAGE:
-                b, t0 = divmod(s * STAGE, TPP)
+        def rope_q(u):
+            t = NT * u % TPP
+            mu = mpool.tile([P, NT, 2, 3, 64], F32, tag="mu", name="mu%d" % u)
+            nc.vector.tensor_tensor(
+                out=mu[:, :, :, 0:2, :],
+                in0=ybank[u][:].rearrange("p t (h d) -> p t h d", h=2).unsqueeze(2).to_broadcast([P, NT, 2, 2, 64]),
+                in1=tab[:, t:t + NT].unsqueeze(3).to_broadcast([P, NT, 2, 2, 64]), op=MULT)
+            mus[u] = mu
+
+        def rope_k(u):
+            t = NT * u % TPP
+            tl = NT * u % STAGE
+            kvs, ys = stage_of(u)
+            nc.vector.tensor_tensor(
+                out=mus[u][:, :, :, 2, :], in0=kvs[:, 0, tl:tl + NT, :].unsqueeze(2).to_broadcast([P, NT, 2, 64]),
+                in1=tab[:, t:t + NT], op=MULT)
+
+        def add(u):
+            tl = NT * u % STAGE
+            kvs, ys = stage_of(u)
+            mu = mus[u]
+            nc.gpsimd.tensor_tensor(
+                out=ys[:, :, tl:tl + NT, :].rearrange("p h t (i e) -> p t h i e", e=2),
+                in0=mu[:, :, 0].rearrange("p t h (i e) -> p t h i e", e=2),
+                in1=mu[:, :, 1].rearrange("p t h (i e) -> p t h i e", e=2)[:, :, :, :, ::-1], op=ADD)
+
+        def store(u):
+            if NT * (u + 1) % STAGE == 0:
+                b, t0 = divmod(NT * (u + 1) - STAGE, TPP)
                 t1 = t0 + STAGE
+                kvs, ys = stage_of(u)
                 nc.sync.dma_start(out=out_2[b, 0].rearrange("(p t) d -> p t d", t=TPP)[:, t0:t1, :],
                                   in_=kvs[:, 1, :, :])
                 nc.sync.dma_start(out=out_1[b, 0].rearrange("(p t) d -> p t d", t=TPP)[:, t0:t1, :],
-                                  in_=ysk[:])
+                                  in_=ys[:, 2, :, :])
                 nc.sync.dma_start(out=out_0[b].rearrange("h (p t) d -> p h t d", t=TPP)[:, :, t0:t1, :],
-                                  in_=ysq[:])
+                                  in_=ys[:, 0:2, :, :])
 
-        transposes(0)
-        copies(0)
-        turn_tab(0)
-        transposes(1)
-        quant(0)
-        copies(1)
-        for k in range(NG):
-            mx(k)
-            if k >= 1:
-                back(k - 1)
-            if k in (1, 2, 3):
-                turn_tab(k)
-            if k + 2 < NG:
-                transposes(k + 2)
-            if k + 1 < NG:
-                quant(k + 1)
-            rope_q(k)
-            kv(k)
-            if k + 2 < NG:
-                copies(k + 2)
-            if k + AHEAD < NG:
-                load_x(k + AHEAD)
-        back(NG - 1)
+        order = [(quant, 2), (transposes, 1), (back, 4), (copies, 1), (mx_q, 3), (bias_q, 3), (mx_kv, 3),
+                 (bias_kv, 4), (rope_q, 4), (rope_k, 4), (add, 4), (store, 4)]
+        depth = max(lag for stage_fn, lag in order)
+        for step in range(NU + depth):
+            for stage_fn, lag in order:
+                u = step - lag
+                if 0 <= u < NU:
+                    stage_fn(u)
+                    if stage_fn is transposes and u == 0:
+                        weights()
+            if step >= 2 and step - 2 + AHEAD < NU:
+                load_x(step - 2 + AHEAD)

@@ -24,6 +24,10 @@ STAGE = 8
 AHEAD = 8
 
 
+def presorted(u):
+    return [0] if u % 2 == 1 and u >= 3 else []
+
+
 def tile_multiqueryattention_pa_t_kernel(tc, tensor, w_qkv, b_qkv, pos_emb, out_0, out_1, out_2):
     nc = tc.nc
     with ExitStack() as ctx:
@@ -102,14 +106,21 @@ def tile_multiqueryattention_pa_t_kernel(tc, tensor, w_qkv, b_qkv, pos_emb, out_
 
         tbank, grp, codes, qbank, kvbank, xqs, ybank, mus, stage, pres = {}, {}, {}, {}, {}, {}, {}, {}, {}, {}
 
+        def presort(u):
+            for i in presorted(u):
+                pt = gpool.tile([P, 2, 2, P], F32, tag="pre", name="pre%d_%d" % (u, i))
+                nc.scalar.copy(out=pt[:],
+                               in_=xsrc[u][:, i, :].bitcast(F32).rearrange("p (g r u) -> p g u r", g=2, u=2))
+                pres[(u, i)] = pt
+
         def transposes(u):
             for i in range(NT):
                 tp = psum.tile([P, 512], F32, tag="T%d" % ((NT * u + i) % 4), name="T%d_%d" % (u, i))
                 xa = xsrc[u][:, i, :].bitcast(F32)
                 for g in range(2):
                     for h in range(2):
-                        nc.tensor.transpose(tp[:, 256 * g + 128 * h:256 * g + 128 * (h + 1)],
-                                            xa[:, 256 * g + h:256 * (g + 1):2], ident_f[:])
+                        src = pres[(u, i)][:, g, h, :] if (u, i) in pres else xa[:, 256 * g + h:256 * (g + 1):2]
+                        nc.tensor.transpose(tp[:, 256 * g + 128 * h:256 * g + 128 * (h + 1)], src, ident_f[:])
                 tbank[(u, i)] = tp
 
         def copies(u):
@@ -218,7 +229,7 @@ def tile_multiqueryattention_pa_t_kernel(tc, tensor, w_qkv, b_qkv, pos_emb, out_
                 nc.sync.dma_start(out=out_0[b].rearrange("h (p t) d -> p h t d", t=TPP)[:, :, t0:t1, :],
                                   in_=ys[:, 0:2, :, :])
 
-        order = [(quant, 2), (transposes, 1), (back, 4), (copies, 1), (mx_q, 3), (bias_q, 3), (mx_kv, 3),
+        order = [(presort, 0), (quant, 2), (transposes, 1), (back, 4), (copies, 1), (mx_q, 3), (bias_q, 3), (mx_kv, 3),
                  (bias_kv, 4), (rope_q, 4), (rope_k, 4), (add, 4), (store, 4)]
         depth = max(lag for stage_fn, lag in order)
         for step in range(NU + depth):

@@ -28,6 +28,13 @@ def presorted(u):
     return [0] if u % 2 == 1 and u >= 3 else []
 
 
+def stored_after(u):
+    last = NT * (u + 1) % STAGE or STAGE
+    if NT * (u + 1) > NB * TPP - STAGE:
+        return {4: (0, 4), 6: (4, 6), 8: (6, 8)}.get(last)
+    return (0, STAGE) if last == STAGE else None
+
+
 def tile_multiqueryattention_pa_t_kernel(tc, tensor, w_qkv, b_qkv, pos_emb, out_0, out_1, out_2):
     nc = tc.nc
     with ExitStack() as ctx:
@@ -40,36 +47,37 @@ def tile_multiqueryattention_pa_t_kernel(tc, tensor, w_qkv, b_qkv, pos_emb, out_
         psum = ctx.enter_context(tc.psum_pool(name="psum", bufs=1))
         ctx.enter_context(tc.manual_schedule())
 
-        bb = const.tile([P, 256], BF16, name="bb")
-        nc.scalar.dma_start(out=bb[:], in_=b_qkv.partition_broadcast(P))
+        brow = const.tile([P, 256], BF16, name="brow")
+        nc.vector.memset(brow[:], 0.0)
         xsrc = {}
 
-        def load_x(u):
+        def load_x(u, pieces=1):
             b, t0 = divmod(u * NT, TPP)
             view = tensor[b].rearrange("(p t) k -> p t k", t=TPP)
             xt = xpool.tile([P, NT, HID], BF16, tag="x", name="x%d" % u)
-            nc.sync.dma_start(out=xt[:], in_=view[:, t0:t0 + NT, :])
+            n = NT // pieces
+            for i in range(0, NT, n):
+                nc.sync.dma_start(out=xt[:, i:i + n, :], in_=view[:, t0 + i:t0 + i + n, :])
             xsrc[u] = xt
 
-        load_x(0)
+        load_x(0, pieces=2)
         w_sb = const.tile([P, 2, HID], BF16, name="w_sb")
-        nc.sync.dma_start(out=w_sb[:], in_=w_qkv.rearrange("(a p) k -> p a k", p=P))
+        for a in range(2):
+            nc.sync.dma_start(out=w_sb[:, a, :], in_=w_qkv[P * a:P * (a + 1), :])
+        nc.scalar.dma_start(out=brow[0:1, :], in_=b_qkv.unsqueeze(0))
         load_x(1)
         pe_sb = const.tile([P, TPP, 128], BF16, name="pe_sb")
         nc.sync.dma_start(out=pe_sb[:], in_=pos_emb.rearrange("(p t) c -> p t c", t=TPP))
-        for u in range(2, AHEAD):
+        for u in range(2, AHEAD + 1):
             load_x(u)
 
         warm = const.tile([P, 2], F32, name="warm")
         nc.vector.memset(warm[:], 0.0)
         nc.scalar.activation(out=warm[:, 0:1], in_=warm[:, 1:2], func=IDENT, bias=0.0, scale=1.0)
+        ones = const.tile([P, P], BF16, name="ones")
+        nc.vector.memset(ones[:], 1.0)
         ident_f = const.tile([P, P], F32, name="ident_f")
         make_identity(nc, ident_f[:])
-
-        bsel = const.tile([P, P], F32, name="bsel")
-        nc.vector.tensor_tensor(out=bsel[:], in0=bb[:, 0:P], in1=ident_f[:], op=MULT)
-        bcol = const.tile([P, 1], F32, name="bcol")
-        nc.vector.tensor_reduce(out=bcol[:], in_=bsel[:], axis=mybir.AxisListType.X, op=ADD)
 
         tab = const.tile([P, TPP, 2, 64], BF16, name="tab")
 
@@ -87,30 +95,44 @@ def tile_multiqueryattention_pa_t_kernel(tc, tensor, w_qkv, b_qkv, pos_emb, out_
         wg = const.tile([P, 2048], BF16, name="wg", align_bytes=64)
         wc = const.tile([P, 512], U32, name="wc", align_bytes=64)
         ws = const.tile([P, 512], U8, name="ws", align_bytes=64)
+        bkv = const.tile([P, P], F32, name="bkv")
+        bcol = const.tile([P, 1], F32, name="bcol")
 
-        def weights():
-            wg_f = wg[:].bitcast(F32).rearrange("p (g n u) -> p g n u", g=2, u=2)
+        wbank, tbank, grp, codes, qbank, kvbank, xqs, ybank, mus, stage, pres = {}, {}, {}, {}, {}, {}, {}, {}, {}, {}, {}
+
+        def weight_transposes():
             for a in range(2):
                 tw = psum.tile([P, 512], F32, tag="T%d" % (2 + a), name="tw%d" % a)
                 wa = w_sb[:, a, :].bitcast(F32)
                 for g in range(2):
-                    for u in range(2):
-                        nc.tensor.transpose(tw[:, 256 * g + 128 * u:256 * g + 128 * (u + 1)],
-                                            wa[:, 256 * g + u:256 * (g + 1):2], ident_f[:])
-                src = tw[:].rearrange("p (g u n) -> p g n u", g=2, u=2)
+                    for h in range(2):
+                        nc.tensor.transpose(tw[:, 256 * g + 128 * h:256 * g + 128 * (h + 1)],
+                                            wa[:, 256 * g + h:256 * (g + 1):2], ident_f[:])
+                wbank[a] = tw
+
+        def bias_spread():
+            bk = psum.tile([P, P], F32, tag="Y", name="bk")
+            nc.tensor.matmul(bk[:], lhsT=ones[:], rhs=brow[:, 128:256], start=True, stop=True)
+            bq = psum.tile([P, 1], F32, tag="Q", name="bq")
+            nc.tensor.matmul(bq[:], lhsT=brow[:, 0:128], rhs=ones[:, 0:1], start=True, stop=True)
+            nc.scalar.copy(out=bcol[:], in_=bq[:])
+            nc.scalar.copy(out=bkv[:], in_=bk[:])
+
+        def weight_quant():
+            wg_f = wg[:].bitcast(F32).rearrange("p (g n u) -> p g n u", g=2, u=2)
+            for a in range(2):
+                src = wbank[a][:].rearrange("p (g u n) -> p g n u", g=2, u=2)
                 if a == 0:
                     nc.scalar.copy(out=wg_f[:, :, 0:128, :], in_=src)
                 else:
                     nc.vector.tensor_copy(out=wg_f[:, :, 128:256, :], in_=src)
             nc.vector.quantize_mx(out=wc[:].bitcast(FP8X4), scales=ws[:], in_=wg[:])
 
-        tbank, grp, codes, qbank, kvbank, xqs, ybank, mus, stage, pres = {}, {}, {}, {}, {}, {}, {}, {}, {}, {}
-
         def presort(u):
             for i in presorted(u):
                 pt = gpool.tile([P, 2, 2, P], F32, tag="pre", name="pre%d_%d" % (u, i))
                 nc.scalar.copy(out=pt[:],
-                               in_=xsrc[u][:, i, :].bitcast(F32).rearrange("p (g r u) -> p g u r", g=2, u=2))
+                               in_=xsrc[u][:, i, :].bitcast(F32).rearrange("p (g r h) -> p g h r", g=2, h=2))
                 pres[(u, i)] = pt
 
         def transposes(u):
@@ -127,7 +149,11 @@ def tile_multiqueryattention_pa_t_kernel(tc, tensor, w_qkv, b_qkv, pos_emb, out_
             gt = gpool.tile([P, NT * HID], BF16, tag="grp", name="grp%d" % u, align_bytes=64)
             gf = gt[:].bitcast(F32).rearrange("p (g i r h) -> p g i r h", g=2, i=NT, h=2)
             for i in range(NT):
-                nc.scalar.copy(out=gf[:, :, i], in_=tbank[(u, i)][:].rearrange("p (g h r) -> p g r h", g=2, h=2))
+                src = tbank[(u, i)][:].rearrange("p (g h r) -> p g r h", g=2, h=2)
+                if u == 0 and i == 1:
+                    nc.vector.tensor_copy(out=gf[:, :, i], in_=src)
+                else:
+                    nc.scalar.copy(out=gf[:, :, i], in_=src)
             grp[u] = gt
 
         def quant(u):
@@ -188,7 +214,7 @@ def tile_multiqueryattention_pa_t_kernel(tc, tensor, w_qkv, b_qkv, pos_emb, out_
             nc.vector.tensor_tensor(
                 out=kvs[:, :, tl:tl + NT, :].rearrange("p h t d -> p t h d"),
                 in0=kvbank[u][:].rearrange("p t (h d) -> p t h d", h=2),
-                in1=bb[:, 128:256].rearrange("p (h d) -> p h d", h=2).unsqueeze(1).to_broadcast([P, NT, 2, 64]),
+                in1=bkv[:].rearrange("p (h d) -> p h d", h=2).unsqueeze(1).to_broadcast([P, NT, 2, 64]),
                 op=ADD)
 
         def rope_q(u):
@@ -212,32 +238,59 @@ def tile_multiqueryattention_pa_t_kernel(tc, tensor, w_qkv, b_qkv, pos_emb, out_
             tl = NT * u % STAGE
             kvs, ys = stage_of(u)
             mu = mus[u]
-            nc.gpsimd.tensor_tensor(
+            engine = nc.vector if u == NU - 1 else nc.gpsimd
+            engine.tensor_tensor(
                 out=ys[:, :, tl:tl + NT, :].rearrange("p h t (i e) -> p t h i e", e=2),
                 in0=mu[:, :, 0].rearrange("p t h (i e) -> p t h i e", e=2),
                 in1=mu[:, :, 1].rearrange("p t h (i e) -> p t h i e", e=2)[:, :, :, :, ::-1], op=ADD)
 
         def store(u):
-            if NT * (u + 1) % STAGE == 0:
-                b, t0 = divmod(NT * (u + 1) - STAGE, TPP)
-                t1 = t0 + STAGE
+            span = stored_after(u)
+            if span:
+                l0, l1 = span
+                b, t0 = divmod(NT * u // STAGE * STAGE, TPP)
+                t0, t1 = t0 + l0, t0 + l1
                 kvs, ys = stage_of(u)
                 nc.sync.dma_start(out=out_2[b, 0].rearrange("(p t) d -> p t d", t=TPP)[:, t0:t1, :],
-                                  in_=kvs[:, 1, :, :])
+                                  in_=kvs[:, 1, l0:l1, :])
                 nc.sync.dma_start(out=out_1[b, 0].rearrange("(p t) d -> p t d", t=TPP)[:, t0:t1, :],
-                                  in_=ys[:, 2, :, :])
+                                  in_=ys[:, 2, l0:l1, :])
                 nc.sync.dma_start(out=out_0[b].rearrange("h (p t) d -> p h t d", t=TPP)[:, :, t0:t1, :],
-                                  in_=ys[:, 0:2, :, :])
+                                  in_=ys[:, 0:2, l0:l1, :])
 
-        order = [(presort, 0), (quant, 2), (transposes, 1), (back, 4), (copies, 1), (mx_q, 3), (bias_q, 3), (mx_kv, 3),
-                 (bias_kv, 4), (rope_q, 4), (rope_k, 4), (add, 4), (store, 4)]
-        depth = max(lag for stage_fn, lag in order)
-        for step in range(NU + depth):
-            for stage_fn, lag in order:
-                u = step - lag
-                if 0 <= u < NU:
-                    stage_fn(u)
-                    if stage_fn is transposes and u == 0:
-                        weights()
-            if step >= 2 and step - 2 + AHEAD < NU:
-                load_x(step - 2 + AHEAD)
+        transposes(0)
+        copies(0)
+        weight_transposes()
+        quant(0)
+        weight_quant()
+        transposes(1)
+        copies(1)
+        bias_spread()
+        for u in range(NU + 1):
+            if u + 3 < NU:
+                presort(u + 3)
+            if u + 1 < NU:
+                quant(u + 1)
+            if u + 2 < NU:
+                transposes(u + 2)
+                back_first = True
+            else:
+                back_first = False
+            if back_first and u >= 1:
+                back(u - 1)
+            if u + 2 < NU:
+                copies(u + 2)
+            if u < NU:
+                mx_q(u)
+                bias_q(u)
+                mx_kv(u)
+            if u >= 1:
+                if not back_first:
+                    back(u - 1)
+                bias_kv(u - 1)
+                rope_q(u - 1)
+                rope_k(u - 1)
+                add(u - 1)
+                store(u - 1)
+            if u + 1 + AHEAD < NU:
+                load_x(u + 1 + AHEAD)

@@ -18,21 +18,23 @@ P = 128
 NB = 4
 TPP = 16
 HID = 1024
+NTILE = NB * TPP
 NT = 2
-NU = NB * TPP // NT
+UNITS = [(NT * i, NT) for i in range(31)] + [(62, 1), (63, 1)]
+NU = len(UNITS)
 STAGE = 8
 AHEAD = 8
 
 
 def presorted(u):
-    return [0] if u % 2 == 1 and u >= 3 else []
+    return [0] if u % 2 == 1 and 7 <= u < NU - 2 else []
 
 
 def stored_after(u):
-    last = NT * (u + 1) % STAGE or STAGE
-    if NT * (u + 1) > NB * TPP - STAGE:
-        return {4: (0, 4), 6: (4, 6), 8: (6, 8)}.get(last)
-    return (0, STAGE) if last == STAGE else None
+    end = sum(UNITS[u])
+    if end > NTILE - STAGE:
+        return {4: (0, 4), 7: (4, 7), 8: (7, 8)}.get(end - NTILE + STAGE)
+    return (0, STAGE) if end % STAGE == 0 else None
 
 
 def tile_multiqueryattention_pa_t_kernel(tc, tensor, w_qkv, b_qkv, pos_emb, out_0, out_1, out_2):
@@ -52,11 +54,12 @@ def tile_multiqueryattention_pa_t_kernel(tc, tensor, w_qkv, b_qkv, pos_emb, out_
         xsrc = {}
 
         def load_x(u, pieces=1):
-            b, t0 = divmod(u * NT, TPP)
+            first, nt = UNITS[u]
+            b, t0 = divmod(first, TPP)
             view = tensor[b].rearrange("(p t) k -> p t k", t=TPP)
-            xt = xpool.tile([P, NT, HID], BF16, tag="x", name="x%d" % u)
-            n = NT // pieces
-            for i in range(0, NT, n):
+            xt = xpool.tile([P, nt, HID], BF16, tag="x", name="x%d" % u)
+            n = nt // pieces
+            for i in range(0, nt, n):
                 nc.sync.dma_start(out=xt[:, i:i + n, :], in_=view[:, t0 + i:t0 + i + n, :])
             xsrc[u] = xt
 
@@ -65,10 +68,17 @@ def tile_multiqueryattention_pa_t_kernel(tc, tensor, w_qkv, b_qkv, pos_emb, out_
         for a in range(2):
             nc.sync.dma_start(out=w_sb[:, a, :], in_=w_qkv[P * a:P * (a + 1), :])
         nc.scalar.dma_start(out=brow[0:1, :], in_=b_qkv.unsqueeze(0))
-        load_x(1)
+        load_x(1, pieces=2)
         pe_sb = const.tile([P, TPP, 128], BF16, name="pe_sb")
-        nc.sync.dma_start(out=pe_sb[:], in_=pos_emb.rearrange("(p t) c -> p t c", t=TPP))
-        for u in range(2, AHEAD + 1):
+
+        def load_pe(ta, tb):
+            nc.sync.dma_start(out=pe_sb[:, ta:tb, :], in_=pos_emb.rearrange("(p t) c -> p t c", t=TPP)[:, ta:tb, :])
+
+        load_pe(0, 4)
+        load_x(2, pieces=2)
+        load_x(3)
+        load_pe(4, TPP)
+        for u in range(4, AHEAD + 1):
             load_x(u)
 
         warm = const.tile([P, 2], F32, name="warm")
@@ -102,7 +112,7 @@ def tile_multiqueryattention_pa_t_kernel(tc, tensor, w_qkv, b_qkv, pos_emb, out_
 
         def weight_transposes():
             for a in range(2):
-                tw = psum.tile([P, 512], F32, tag="T%d" % (2 + a), name="tw%d" % a)
+                tw = psum.tile([P, 512], F32, tag="KV%d" % a, name="tw%d" % a)
                 wa = w_sb[:, a, :].bitcast(F32)
                 for g in range(2):
                     for h in range(2):
@@ -136,8 +146,9 @@ def tile_multiqueryattention_pa_t_kernel(tc, tensor, w_qkv, b_qkv, pos_emb, out_
                 pres[(u, i)] = pt
 
         def transposes(u):
-            for i in range(NT):
-                tp = psum.tile([P, 512], F32, tag="T%d" % ((NT * u + i) % 4), name="T%d_%d" % (u, i))
+            first, nt = UNITS[u]
+            for i in range(nt):
+                tp = psum.tile([P, 512], F32, tag="T%d" % ((first + i) % 4), name="T%d_%d" % (u, i))
                 xa = xsrc[u][:, i, :].bitcast(F32)
                 for g in range(2):
                     for h in range(2):
@@ -146,26 +157,29 @@ def tile_multiqueryattention_pa_t_kernel(tc, tensor, w_qkv, b_qkv, pos_emb, out_
                 tbank[(u, i)] = tp
 
         def copies(u):
-            gt = gpool.tile([P, NT * HID], BF16, tag="grp", name="grp%d" % u, align_bytes=64)
-            gf = gt[:].bitcast(F32).rearrange("p (g i r h) -> p g i r h", g=2, i=NT, h=2)
-            for i in range(NT):
+            first, nt = UNITS[u]
+            gt = gpool.tile([P, nt * HID], BF16, tag="grp", name="grp%d" % u, align_bytes=64)
+            gf = gt[:].bitcast(F32).rearrange("p (g i r h) -> p g i r h", g=2, i=nt, h=2)
+            for i in range(nt):
                 src = tbank[(u, i)][:].rearrange("p (g h r) -> p g r h", g=2, h=2)
-                if u == 0 and i == 1:
+                if u <= 1 and i == 1:
                     nc.vector.tensor_copy(out=gf[:, :, i], in_=src)
                 else:
                     nc.scalar.copy(out=gf[:, :, i], in_=src)
             grp[u] = gt
 
         def quant(u):
-            c = cpool.tile([P, NT * 256], U32, tag="codes", name="codes%d" % u, align_bytes=64)
-            s = cpool.tile([P, NT * 256], U8, tag="scl", name="scl%d" % u, align_bytes=64)
+            first, nt = UNITS[u]
+            c = cpool.tile([P, nt * 256], U32, tag="codes", name="codes%d" % u, align_bytes=64)
+            s = cpool.tile([P, nt * 256], U8, tag="scl", name="scl%d" % u, align_bytes=64)
             nc.vector.quantize_mx(out=c[:].bitcast(FP8X4), scales=s[:], in_=grp[u][:])
             codes[u] = (c, s)
 
         def mx_q(u):
             c, s = codes[u]
-            w = NT * P
-            qb = psum.tile([P, w], F32, tag="Q", name="Q%d" % u)
+            first, nt = UNITS[u]
+            w = nt * P
+            qb = psum.tile([P, w], F32, tag="T1" if u == NU - 1 else "Q", name="Q_%d" % u)
             for g in range(2):
                 nc.tensor.matmul_mx(
                     out=qb[:],
@@ -176,9 +190,10 @@ def tile_multiqueryattention_pa_t_kernel(tc, tensor, w_qkv, b_qkv, pos_emb, out_
 
         def mx_kv(u):
             c, s = codes[u]
-            w = NT * P
-            kvb = psum.tile([P, NT, P], F32, tag="KV%d" % (u % 2), name="KV_%d" % u)
-            for i in range(NT):
+            first, nt = UNITS[u]
+            w = nt * P
+            kvb = psum.tile([P, nt, P], F32, tag="KV%d" % (u % 2), name="KV_%d" % u)
+            for i in range(nt):
                 for g in range(2):
                     lo = w * g + P * i
                     nc.tensor.matmul_mx(
@@ -190,18 +205,20 @@ def tile_multiqueryattention_pa_t_kernel(tc, tensor, w_qkv, b_qkv, pos_emb, out_
             kvbank[u] = kvb
 
         def bias_q(u):
-            xq = mpool.tile([P, NT * P], F32, tag="xq", name="xq%d" % u)
+            first, nt = UNITS[u]
+            xq = mpool.tile([P, nt * P], F32, tag="xq", name="xq%d" % u)
             nc.scalar.activation(out=xq[:], in_=qbank[u][:], func=IDENT, bias=bcol[:, 0:1], scale=1.0)
             xqs[u] = xq
 
         def back(u):
-            yb = psum.tile([P, NT, P], F32, tag="Y", name="Y%d" % u)
-            for i in range(NT):
+            first, nt = UNITS[u]
+            yb = psum.tile([P, nt, P], F32, tag="T0" if u == NU - 1 else "Y", name="Y_%d" % u)
+            for i in range(nt):
                 nc.tensor.transpose(yb[:, i, :], xqs[u][:, P * i:P * (i + 1)], ident_f[:])
             ybank[u] = yb
 
         def stage_of(u):
-            s = NT * u // STAGE
+            s = UNITS[u][0] // STAGE
             if s not in stage:
                 kvs = ypool.tile([P, 2, STAGE, 64], F32, tag="kvs", name="kvs%d" % s)
                 ys = ypool.tile([P, 3, STAGE, 64], F32, tag="ys", name="ys%d" % s)
@@ -209,38 +226,42 @@ def tile_multiqueryattention_pa_t_kernel(tc, tensor, w_qkv, b_qkv, pos_emb, out_
             return stage[s]
 
         def bias_kv(u):
-            tl = NT * u % STAGE
+            first, nt = UNITS[u]
+            tl = first % STAGE
             kvs, ys = stage_of(u)
             nc.vector.tensor_tensor(
-                out=kvs[:, :, tl:tl + NT, :].rearrange("p h t d -> p t h d"),
+                out=kvs[:, :, tl:tl + nt, :].rearrange("p h t d -> p t h d"),
                 in0=kvbank[u][:].rearrange("p t (h d) -> p t h d", h=2),
-                in1=bkv[:].rearrange("p (h d) -> p h d", h=2).unsqueeze(1).to_broadcast([P, NT, 2, 64]),
+                in1=bkv[:].rearrange("p (h d) -> p h d", h=2).unsqueeze(1).to_broadcast([P, nt, 2, 64]),
                 op=ADD)
 
         def rope_q(u):
-            t = NT * u % TPP
-            mu = mpool.tile([P, NT, 2, 3, 64], F32, tag="mu", name="mu%d" % u)
+            t = UNITS[u][0] % TPP
+            nt = UNITS[u][1]
+            mu = mpool.tile([P, nt, 2, 3, 64], F32, tag="mu", name="mu%d" % u)
             nc.vector.tensor_tensor(
                 out=mu[:, :, :, 0:2, :],
-                in0=ybank[u][:].rearrange("p t (h d) -> p t h d", h=2).unsqueeze(2).to_broadcast([P, NT, 2, 2, 64]),
-                in1=tab[:, t:t + NT].unsqueeze(3).to_broadcast([P, NT, 2, 2, 64]), op=MULT)
+                in0=ybank[u][:].rearrange("p t (h d) -> p t h d", h=2).unsqueeze(2).to_broadcast([P, nt, 2, 2, 64]),
+                in1=tab[:, t:t + nt].unsqueeze(3).to_broadcast([P, nt, 2, 2, 64]), op=MULT)
             mus[u] = mu
 
         def rope_k(u):
-            t = NT * u % TPP
-            tl = NT * u % STAGE
+            t = UNITS[u][0] % TPP
+            first, nt = UNITS[u]
+            tl = first % STAGE
             kvs, ys = stage_of(u)
             nc.vector.tensor_tensor(
-                out=mus[u][:, :, :, 2, :], in0=kvs[:, 0, tl:tl + NT, :].unsqueeze(2).to_broadcast([P, NT, 2, 64]),
-                in1=tab[:, t:t + NT], op=MULT)
+                out=mus[u][:, :, :, 2, :], in0=kvs[:, 0, tl:tl + nt, :].unsqueeze(2).to_broadcast([P, nt, 2, 64]),
+                in1=tab[:, t:t + nt], op=MULT)
 
         def add(u):
-            tl = NT * u % STAGE
+            first, nt = UNITS[u]
+            tl = first % STAGE
             kvs, ys = stage_of(u)
             mu = mus[u]
             engine = nc.vector if u == NU - 1 else nc.gpsimd
             engine.tensor_tensor(
-                out=ys[:, :, tl:tl + NT, :].rearrange("p h t (i e) -> p t h i e", e=2),
+                out=ys[:, :, tl:tl + nt, :].rearrange("p h t (i e) -> p t h i e", e=2),
                 in0=mu[:, :, 0].rearrange("p t h (i e) -> p t h i e", e=2),
                 in1=mu[:, :, 1].rearrange("p t h (i e) -> p t h i e", e=2)[:, :, :, :, ::-1], op=ADD)
 
@@ -248,7 +269,7 @@ def tile_multiqueryattention_pa_t_kernel(tc, tensor, w_qkv, b_qkv, pos_emb, out_
             span = stored_after(u)
             if span:
                 l0, l1 = span
-                b, t0 = divmod(NT * u // STAGE * STAGE, TPP)
+                b, t0 = divmod(UNITS[u][0] // STAGE * STAGE, TPP)
                 t0, t1 = t0 + l0, t0 + l1
                 kvs, ys = stage_of(u)
                 nc.sync.dma_start(out=out_2[b, 0].rearrange("(p t) d -> p t d", t=TPP)[:, t0:t1, :],

from contextlib import ExitStack

import concourse.mybir as mybir
from concourse.masks import make_identity

FLOPS = 2 * 8192 * 1024 * 256

F32 = mybir.dt.float32
BF16 = mybir.dt.bfloat16
U32 = mybir.dt.uint32
U8 = mybir.dt.uint8
FP8X4 = mybir.dt.float8_e4m3fn_x4
ADD = mybir.AluOpType.add
MULT = mybir.AluOpType.mult
IDENT = mybir.ActivationFunctionType.Identity

P = 128
NB = 4
TPP = 16
HID = 1024
NTILE = NB * TPP
NT = 2
UNITS = [(NT * i, NT) for i in range(31)] + [(62, 1), (63, 1)]
NU = len(UNITS)
STAGE = 8
AHEAD = 8


def presorted(u):
    return [0] if u % 2 == 1 and 7 <= u < NU - 2 else []


def stored_after(u):
    end = sum(UNITS[u])
    if end > NTILE - STAGE:
        return {4: (0, 4), 7: (4, 7), 8: (7, 8)}.get(end - NTILE + STAGE)
    return (0, STAGE) if end % STAGE == 0 else None


def tile_multiqueryattention_pa_t_kernel(tc, tensor, w_qkv, b_qkv, pos_emb, out_0, out_1, out_2):
    nc = tc.nc
    with ExitStack() as ctx:
        const = ctx.enter_context(tc.tile_pool(name="const", bufs=1))
        xpool = ctx.enter_context(tc.tile_pool(name="xpool", bufs=12))
        gpool = ctx.enter_context(tc.tile_pool(name="gpool", bufs=3))
        cpool = ctx.enter_context(tc.tile_pool(name="cpool", bufs=2))
        mpool = ctx.enter_context(tc.tile_pool(name="mpool", bufs=3))
        ypool = ctx.enter_context(tc.tile_pool(name="ypool", bufs=3))
        psum = ctx.enter_context(tc.psum_pool(name="psum", bufs=1))
        ctx.enter_context(tc.manual_schedule())

        brow = const.tile([P, 256], BF16, name="brow")
        nc.vector.memset(brow[:], 0.0)
        xsrc = {}

        def load_x(u, pieces=1):
            first, nt = UNITS[u]
            b, t0 = divmod(first, TPP)
            view = tensor[b].rearrange("(p t) k -> p t k", t=TPP)
            xt = xpool.tile([P, nt, HID], BF16, tag="x", name="x%d" % u)
            n = nt // pieces
            for i in range(0, nt, n):
                nc.sync.dma_start(out=xt[:, i:i + n, :], in_=view[:, t0 + i:t0 + i + n, :])
            xsrc[u] = xt

        load_x(0, pieces=2)
        w_sb = const.tile([P, 2, HID], BF16, name="w_sb")
        for a in range(2):
            nc.sync.dma_start(out=w_sb[:, a, :], in_=w_qkv[P * a:P * (a + 1), :])
        nc.scalar.dma_start(out=brow[0:1, :], in_=b_qkv.unsqueeze(0))
        load_x(1, pieces=2)
        pe_sb = const.tile([P, TPP, 128], BF16, name="pe_sb")

        def load_pe(ta, tb):
            nc.sync.dma_start(out=pe_sb[:, ta:tb, :], in_=pos_emb.rearrange("(p t) c -> p t c", t=TPP)[:, ta:tb, :])

        load_pe(0, 4)
        load_x(2, pieces=2)
        load_x(3)
        load_pe(4, TPP)
        for u in range(4, AHEAD + 1):
            load_x(u)

        warm = const.tile([P, 2], F32, name="warm")
        nc.vector.memset(warm[:], 0.0)
        nc.scalar.activation(out=warm[:, 0:1], in_=warm[:, 1:2], func=IDENT, bias=0.0, scale=1.0)
        ones = const.tile([P, P], BF16, name="ones")
        nc.vector.memset(ones[:], 1.0)
        ident_f = const.tile([P, P], F32, name="ident_f")
        make_identity(nc, ident_f[:])

        tab = const.tile([P, TPP, 2, 64], BF16, name="tab")

        def build_tab(ta, tb):
            nc.gpsimd.tensor_scalar(out=tab[:, ta:tb, 0, :], in0=pe_sb[:, ta:tb, 0:64],
                                    scalar1=1.0, scalar2=0.0, op0=MULT, op1=ADD)
            nc.gpsimd.tensor_scalar(
                out=tab[:, ta:tb, 1, :].rearrange("p t (i e) -> p t i e", e=2),
                in0=pe_sb[:, ta:tb, 64:128].rearrange("p t (i e) -> p t i e", e=2)[:, :, :, ::-1],
                scalar1=1.0, scalar2=0.0, op0=MULT, op1=ADD)

        build_tab(0, 4)
        build_tab(4, TPP)

        wg = const.tile([P, 2048], BF16, name="wg", align_bytes=64)
        wc = const.tile([P, 512], U32, name="wc", align_bytes=64)
        ws = const.tile([P, 512], U8, name="ws", align_bytes=64)
        bkv = const.tile([P, P], F32, name="bkv")
        bcol = const.tile([P, 1], F32, name="bcol")

        wbank, tbank, grp, codes, qbank, kvbank, xqs, ybank, mus, stage, pres = {}, {}, {}, {}, {}, {}, {}, {}, {}, {}, {}

        def weight_transposes():
            for a in range(2):
                tw = psum.tile([P, 512], F32, tag="KV%d" % a, name="tw%d" % a)
                wa = w_sb[:, a, :].bitcast(F32)
                for g in range(2):
                    for h in range(2):
                        nc.tensor.transpose(tw[:, 256 * g + 128 * h:256 * g + 128 * (h + 1)],
                                            wa[:, 256 * g + h:256 * (g + 1):2], ident_f[:])
                wbank[a] = tw

        def bias_spread():
            bk = psum.tile([P, P], F32, tag="Y", name="bk")
            nc.tensor.matmul(bk[:], lhsT=ones[:], rhs=brow[:, 128:256], start=True, stop=True)
            bq = psum.tile([P, 1], F32, tag="Q", name="bq")
            nc.tensor.matmul(bq[:], lhsT=brow[:, 0:128], rhs=ones[:, 0:1], start=True, stop=True)
            nc.scalar.copy(out=bcol[:], in_=bq[:])
            nc.scalar.copy(out=bkv[:], in_=bk[:])

        def weight_quant():
            wg_f = wg[:].bitcast(F32).rearrange("p (g n u) -> p g n u", g=2, u=2)
            for a in range(2):
                src = wbank[a][:].rearrange("p (g u n) -> p g n u", g=2, u=2)
                if a == 0:
                    nc.scalar.copy(out=wg_f[:, :, 0:128, :], in_=src)
                else:
                    nc.vector.tensor_copy(out=wg_f[:, :, 128:256, :], in_=src)
            nc.vector.quantize_mx(out=wc[:].bitcast(FP8X4), scales=ws[:], in_=wg[:])

        def presort(u):
            for i in presorted(u):
                pt = gpool.tile([P, 2, 2, P], F32, tag="pre", name="pre%d_%d" % (u, i))
                nc.scalar.copy(out=pt[:],
                               in_=xsrc[u][:, i, :].bitcast(F32).rearrange("p (g r h) -> p g h r", g=2, h=2))
                pres[(u, i)] = pt

        def transposes(u):
            first, nt = UNITS[u]
            for i in range(nt):
                tp = psum.tile([P, 512], F32, tag="T%d" % ((first + i) % 4), name="T%d_%d" % (u, i))
                xa = xsrc[u][:, i, :].bitcast(F32)
                for g in range(2):
                    for h in range(2):
                        src = pres[(u, i)][:, g, h, :] if (u, i) in pres else xa[:, 256 * g + h:256 * (g + 1):2]
                        nc.tensor.transpose(tp[:, 256 * g + 128 * h:256 * g + 128 * (h + 1)], src, ident_f[:])
                tbank[(u, i)] = tp

        def copies(u):
            first, nt = UNITS[u]
            gt = gpool.tile([P, nt * HID], BF16, tag="grp", name="grp%d" % u, align_bytes=64)
            gf = gt[:].bitcast(F32).rearrange("p (g i r h) -> p g i r h", g=2, i=nt, h=2)
            for i in range(nt):
                src = tbank[(u, i)][:].rearrange("p (g h r) -> p g r h", g=2, h=2)
                if u <= 1 and i == 1:
                    nc.vector.tensor_copy(out=gf[:, :, i], in_=src)
                else:
                    nc.scalar.copy(out=gf[:, :, i], in_=src)
            grp[u] = gt

        def quant(u):
            first, nt = UNITS[u]
            c = cpool.tile([P, nt * 256], U32, tag="codes", name="codes%d" % u, align_bytes=64)
            s = cpool.tile([P, nt * 256], U8, tag="scl", name="scl%d" % u, align_bytes=64)
            nc.vector.quantize_mx(out=c[:].bitcast(FP8X4), scales=s[:], in_=grp[u][:])
            codes[u] = (c, s)

        def mx_q(u):
            c, s = codes[u]
            first, nt = UNITS[u]
            w = nt * P
            qb = psum.tile([P, w], F32, tag="T1" if u == NU - 1 else "Q", name="Q_%d" % u)
            for g in range(2):
                nc.tensor.matmul_mx(
                    out=qb[:],
                    lhsT=wc[:, 256 * g:256 * g + 128].bitcast(FP8X4), lhsT_scale=ws[:, 256 * g:256 * g + 128],
                    rhs=c[:, w * g:w * (g + 1)].bitcast(FP8X4), rhs_scale=s[:, w * g:w * (g + 1)],
                    start=(g == 0), stop=(g == 1))
            qbank[u] = qb

        def mx_kv(u):
            c, s = codes[u]
            first, nt = UNITS[u]
            w = nt * P
            kvb = psum.tile([P, nt, P], F32, tag="KV%d" % (u % 2), name="KV_%d" % u)
            for i in range(nt):
                for g in range(2):
                    lo = w * g + P * i
                    nc.tensor.matmul_mx(
                        out=kvb[:, i, :],
                        lhsT=c[:, lo:lo + P].bitcast(FP8X4), lhsT_scale=s[:, lo:lo + P],
                        rhs=wc[:, 256 * g + 128:256 * (g + 1)].bitcast(FP8X4),
                        rhs_scale=ws[:, 256 * g + 128:256 * (g + 1)],
                        start=(g == 0), stop=(g == 1))
            kvbank[u] = kvb

        def bias_q(u):
            first, nt = UNITS[u]
            xq = mpool.tile([P, nt * P], F32, tag="xq", name="xq%d" % u)
            nc.scalar.activation(out=xq[:], in_=qbank[u][:], func=IDENT, bias=bcol[:, 0:1], scale=1.0)
            xqs[u] = xq

        def back(u):
            first, nt = UNITS[u]
            yb = psum.tile([P, nt, P], F32, tag="T0" if u == NU - 1 else "Y", name="Y_%d" % u)
            for i in range(nt):
                nc.tensor.transpose(yb[:, i, :], xqs[u][:, P * i:P * (i + 1)], ident_f[:])
            ybank[u] = yb

        def stage_of(u):
            s = UNITS[u][0] // STAGE
            if s not in stage:
                kvs = ypool.tile([P, 2, STAGE, 64], F32, tag="kvs", name="kvs%d" % s)
                ys = ypool.tile([P, 3, STAGE, 64], F32, tag="ys", name="ys%d" % s)
                stage[s] = (kvs, ys)
            return stage[s]

        def bias_kv(u):
            first, nt = UNITS[u]
            tl = first % STAGE
            kvs, ys = stage_of(u)
            nc.vector.tensor_tensor(
                out=kvs[:, :, tl:tl + nt, :].rearrange("p h t d -> p t h d"),
                in0=kvbank[u][:].rearrange("p t (h d) -> p t h d", h=2),
                in1=bkv[:].rearrange("p (h d) -> p h d", h=2).unsqueeze(1).to_broadcast([P, nt, 2, 64]),
                op=ADD)

        def rope_q(u):
            t = UNITS[u][0] % TPP
            nt = UNITS[u][1]
            mu = mpool.tile([P, nt, 2, 3, 64], F32, tag="mu", name="mu%d" % u)
            nc.vector.tensor_tensor(
                out=mu[:, :, :, 0:2, :],
                in0=ybank[u][:].rearrange("p t (h d) -> p t h d", h=2).unsqueeze(2).to_broadcast([P, nt, 2, 2, 64]),
                in1=tab[:, t:t + nt].unsqueeze(3).to_broadcast([P, nt, 2, 2, 64]), op=MULT)
            mus[u] = mu

        def rope_k(u):
            t = UNITS[u][0] % TPP
            first, nt = UNITS[u]
            tl = first % STAGE
            kvs, ys = stage_of(u)
            nc.vector.tensor_tensor(
                out=mus[u][:, :, :, 2, :], in0=kvs[:, 0, tl:tl + nt, :].unsqueeze(2).to_broadcast([P, nt, 2, 64]),
                in1=tab[:, t:t + nt], op=MULT)

        def add(u):
            first, nt = UNITS[u]
            tl = first % STAGE
            kvs, ys = stage_of(u)
            mu = mus[u]
            engine = nc.vector if u == NU - 1 else nc.gpsimd
            engine.tensor_tensor(
                out=ys[:, :, tl:tl + nt, :].rearrange("p h t (i e) -> p t h i e", e=2),
                in0=mu[:, :, 0].rearrange("p t h (i e) -> p t h i e", e=2),
                in1=mu[:, :, 1].rearrange("p t h (i e) -> p t h i e", e=2)[:, :, :, :, ::-1], op=ADD)

        def store(u):
            span = stored_after(u)
            if span:
                l0, l1 = span
                b, t0 = divmod(UNITS[u][0] // STAGE * STAGE, TPP)
                t0, t1 = t0 + l0, t0 + l1
                kvs, ys = stage_of(u)
                nc.sync.dma_start(out=out_2[b, 0].rearrange("(p t) d -> p t d", t=TPP)[:, t0:t1, :],
                                  in_=kvs[:, 1, l0:l1, :])
                nc.sync.dma_start(out=out_1[b, 0].rearrange("(p t) d -> p t d", t=TPP)[:, t0:t1, :],
                                  in_=ys[:, 2, l0:l1, :])
                nc.sync.dma_start(out=out_0[b].rearrange("h (p t) d -> p h t d", t=TPP)[:, :, t0:t1, :],
                                  in_=ys[:, 0:2, l0:l1, :])

        transposes(0)
        copies(0)
        weight_transposes()
        quant(0)
        weight_quant()
        transposes(1)
        copies(1)
        bias_spread()
        for u in range(NU + 1):
            if u + 3 < NU:
                presort(u + 3)
            if u + 1 < NU:
                quant(u + 1)
            if u + 2 < NU:
                transposes(u + 2)
                back_first = True
            else:
                back_first = False
            if back_first and u >= 1:
                back(u - 1)
            if u + 2 < NU:
                copies(u + 2)
            if u < NU:
                mx_q(u)
                bias_q(u)
                mx_kv(u)
            if u >= 1:
                if not back_first:
                    back(u - 1)
                bias_kv(u - 1)
                rope_q(u - 1)
                rope_k(u - 1)
                add(u - 1)
                store(u - 1)
            if u + 1 + AHEAD < NU:
                load_x(u + 1 + AHEAD)
